import numpy as np
import ml_dtypes


def mxq(x, axis, fmt="e4m3"):
    dtype, down = {"e4m3": (ml_dtypes.float8_e4m3fn, 7), "e5m2": (ml_dtypes.float8_e5m2, 14)}[fmt]
    v = np.moveaxis(np.asarray(x, np.float32).astype(ml_dtypes.bfloat16).astype(np.float64), axis, -1)
    blocks = v.reshape(v.shape[:-1] + (-1, 32))
    amax = np.abs(blocks).max(-1, keepdims=True)
    byte = np.maximum(np.where(amax > 0, np.frexp(amax)[1] - 1 + 127, 0) - down, 1)
    scale = np.exp2(byte - 127.0)
    codes = (blocks / scale).astype(np.float32).astype(dtype).astype(np.float64)
    return np.moveaxis((codes * scale).reshape(v.shape), -1, axis)


WIDE = False


def mx_kscale(k):
    if not WIDE:
        return np.ones(k)
    levels = np.array([18, -18])
    if k % 512:
        return np.exp2(np.random.permutation(np.resize(levels, k // 32))).repeat(32)
    a = np.empty((k // 512, 16))
    for p in range(k // 512):
        a[p, :8] = np.random.permutation(np.resize(levels, 8))
        for g in range(8):
            far = levels[np.abs(levels - a[p, g]) >= 10]
            a[p, g + 8] = far[np.random.randint(len(far))]
    return np.exp2(a.ravel()).repeat(32)


BF16 = ml_dtypes.bfloat16


def bf(x):
    return np.asarray(x, np.float32).astype(BF16)


def f64(x):
    return np.asarray(x).astype(np.float64)


B, S, DIM, H, NOPE, ROPE, VHD, KV_RANK = 2, 256, 2048, 16, 128, 64, 128, 512
QKHD = NOPE + ROPE
HALF = ROPE // 2
EPS = 1e-5
T = B * S
HN, HR, HV = H * NOPE, H * ROPE, H * VHD


def rope(u, cos, sin):
    ur = u.reshape(u.shape[:-1] + (HALF, 2))
    a, b = ur[..., 0], ur[..., 1]
    c = cos[None, :, None, :]
    s = sin[None, :, None, :]
    return np.stack([a * c - b * s, a * s + b * c], axis=-1).reshape(u.shape)


def rope_back(g, cos, sin):
    gr = g.reshape(g.shape[:-1] + (HALF, 2))
    p, q = gr[..., 0], gr[..., 1]
    c = cos[None, :, None, :]
    s = sin[None, :, None, :]
    return np.stack([p * c + q * s, q * c - p * s], axis=-1).reshape(g.shape)


def setup_inputs():
    s = mx_kscale(T).reshape(B, S, 1)
    u = mx_kscale(HN + HV)
    v = mx_kscale(HR + KV_RANK)
    vr = v[:HR] / np.max(v[:HR])
    vc = v[HR:] / np.min(v[HR:])
    vw = np.concatenate([vr, vc])
    f0 = np.concatenate([u[:HN], vr]).reshape(H, QKHD)
    f1 = u[HN:].reshape(H, VHD)
    inv_freq = 1.0 / 10000.0 ** (np.arange(0, ROPE, 2) / ROPE)
    ang = np.arange(S)[:, None] * inv_freq[None, :]
    x0 = bf(np.random.standard_normal((B, S, DIM)))
    wa0 = bf(np.random.standard_normal((DIM, KV_RANK + HR)) / np.sqrt(DIM))
    ba = bf(np.random.standard_normal(KV_RANK + HR) * 0.2)
    kvn_g = bf(1.0 + 0.1 * np.random.standard_normal(KV_RANK))
    kvn_b = bf(0.1 * np.random.standard_normal(KV_RANK))
    wk0 = bf(np.random.standard_normal((KV_RANK, HN)) / np.sqrt(KV_RANK))
    wk_b = bf(np.random.standard_normal(HN) * 0.2)
    wv0 = bf(np.random.standard_normal((KV_RANK, HV)) / np.sqrt(KV_RANK))
    wv_b = bf(np.random.standard_normal(HV) * 0.2)
    g0 = np.random.standard_normal((B, S, H, QKHD)) * np.exp2(np.random.randint(-6, 1, (B, S, 1, 1)))
    g1 = np.random.standard_normal((B, S, H, VHD)) * np.exp2(np.random.randint(-6, 1, (B, S, 1, 1)))
    c = (f64(x0) @ f64(wa0) + f64(ba))[..., HR:]
    mu = c.mean(-1, keepdims=True)
    rstd = 1.0 / np.sqrt(np.square(c - mu).mean(-1, keepdims=True) + EPS)
    return {"x": bf(f64(x0) * s),
            "wkv_a_w": bf(f64(wa0) / vw),
            "wkv_a_b": ba,
            "kvn_g": kvn_g,
            "kvn_b": kvn_b,
            "wk_w": bf(f64(wk0) / u[:HN]),
            "wk_b": wk_b,
            "wv_w": bf(f64(wv0) / u[HN:]),
            "wv_b": wv_b,
            "cos": bf(np.cos(ang)), "sin": bf(np.sin(ang)),
            "c_lat": np.asarray(c, np.float32),
            "mu": np.asarray(mu, np.float32),
            "rstd": np.asarray(rstd, np.float32),
            "grad_0": bf(g0 * f0 / s[..., None]),
            "grad_1": bf(g1 * f1 / s[..., None])}


def reference(x, wkv_a_w, wkv_a_b, kvn_g, kvn_b, wk_w, wk_b, wv_w, wv_b, cos, sin, c_lat, mu, rstd, grad_0, grad_1):
    g0 = f64(grad_0)
    dk = np.concatenate([g0[..., :NOPE], rope_back(g0[..., NOPE:], f64(cos), f64(sin))], axis=-1).reshape(T, H * QKHD)
    dk_rope = dk[:, HN:]
    dz2 = np.concatenate([dk[:, :HN], f64(grad_1).reshape(T, HV)], axis=1)
    w2 = np.concatenate([f64(wk_w), f64(wv_w)], axis=1)
    dcn = mxq(dz2, 1, "e5m2") @ mxq(w2, 1, "e4m3").T
    r = f64(rstd).reshape(T, 1)
    xhat = (f64(c_lat).reshape(T, KV_RANK) - f64(mu).reshape(T, 1)) * r
    e = dcn * f64(kvn_g)
    dc = r * (e - e.mean(-1, keepdims=True) - xhat * (e * xhat).mean(-1, keepdims=True))
    dz1 = np.concatenate([dk_rope, dc], axis=1)
    dx = mxq(dz1, 1, "e5m2") @ mxq(f64(wkv_a_w), 1, "e4m3").T
    dw = mxq(f64(x).reshape(T, DIM), 0, "e4m3").T @ mxq(dz1, 0, "e5m2")
    return dx.reshape(B, S, DIM), dw

@@ -1,0 +1,364 @@
+from contextlib import ExitStack
+
+import concourse.mybir as mybir
+from concourse.masks import make_identity
+
+F32 = mybir.dt.float32
+BF16 = mybir.dt.bfloat16
+U32 = mybir.dt.uint32
+U8 = mybir.dt.uint8
+E4 = mybir.dt.float8_e4m3fn_x4
+E5 = mybir.dt.float8_e5m2_x4
+MULT = mybir.AluOpType.mult
+ADD = mybir.AluOpType.add
+SUB = mybir.AluOpType.subtract
+
+T, DIM, R, HN, HV, HR, W = 512, 2048, 512, 2048, 2048, 1024, 1536
+FLOPS = 2 * (T * (HN + HV) * R + 2 * T * W * DIM)
+BYTES = 2 * (T * DIM + DIM * W + R * (HN + HV) + T * (HN + HR + HV) + 256 * 64 + R) + 4 * (T * R + 2 * T) + 4 * (T * DIM + DIM * W)
+
+
+def tile_mla_pa_v_kernel(
+    tc, x, wkv_a_w, wkv_a_b, kvn_g, kvn_b, wk_w, wk_b, wv_w, wv_b, cos, sin, c_lat, mu, rstd, grad_0, grad_1, out_0, out_1
+):
+    nc = tc.nc
+    xv = x.flatten_outer_dims().rearrange("(p j) w -> p j w", j=4)
+    g0v = grad_0.rearrange("b s h d -> (b s) (h d)").rearrange("(p j) w -> p j w", j=4)
+    g1v = grad_1.rearrange("b s h d -> (b s) (h d)").rearrange("(p j) w -> p j w", j=4)
+    cv = c_lat.flatten_outer_dims().rearrange("(p j) w -> p j w", j=4)
+    muv = mu.flatten_outer_dims().rearrange("(p j) o -> p (j o)", j=4)
+    rv = rstd.flatten_outer_dims().rearrange("(p j) o -> p (j o)", j=4)
+    cosv = cos.rearrange("(q j) w -> q j w", j=4)
+    sinv = sin.rearrange("(q j) w -> q j w", j=4)
+    o0v = out_0.flatten_outer_dims().rearrange("(p j) w -> p j w", j=4)
+    o1v = out_1.rearrange("(m p) w -> p m w", p=128)
+
+    with ExitStack() as ctx:
+        keep = ctx.enter_context(tc.tile_pool(name="keep", bufs=1))
+        rawp = ctx.enter_context(tc.tile_pool(name="rawp", bufs=10))
+        big = ctx.enter_context(tc.tile_pool(name="big", bufs=5))
+        stgp = ctx.enter_context(tc.tile_pool(name="stgp", bufs=6))
+        work = ctx.enter_context(tc.tile_pool(name="work", bufs=2))
+        ps = ctx.enter_context(tc.psum_pool(name="ps", bufs=3))
+
+        def kt(name, shape, dt):
+            return keep.tile(shape, dt, name=name, align_bytes=64)
+
+        ident = kt("ident", [128, 128], F32)
+        make_identity(nc, ident[:])
+        ones = kt("ones", [128, 128], BF16)
+        nc.gpsimd.memset(ones[:], 1.0)
+        gz = kt("gz", [128, R], BF16)
+        nc.gpsimd.memset(gz[:], 0.0)
+        cosb = kt("cosb", [128, 4, 32], BF16)
+        sinb = kt("sinb", [128, 4, 32], BF16)
+        for h in range(2):
+            nc.scalar.dma_start(out=cosb[64 * h : 64 * h + 64], in_=cosv)
+            nc.scalar.dma_start(out=sinb[64 * h : 64 * h + 64], in_=sinv)
+        mut = kt("mut", [128, 4], F32)
+        rt = kt("rt", [128, 4], F32)
+        nc.scalar.dma_start(out=mut[:], in_=muv)
+        nc.scalar.dma_start(out=rt[:], in_=rv)
+        nc.scalar.dma_start(out=gz[0:1, :], in_=kvn_g.rearrange("(o w) -> o w", o=1))
+
+        w2c = kt("w2c", [128, 8, R], U32)
+        w2s = kt("w2s", [128, 8, R], U8)
+        xc = kt("xc", [128, DIM], U32)
+        xs = kt("xs", [128, DIM], U8)
+        kc = kt("kc", [128, 3, DIM], U32)
+        ks = kt("ks", [128, 3, DIM], U8)
+        tcod = kt("tcod", [128, W], U32)
+        tsc = kt("tsc", [128, W], U8)
+        fc = kt("fc", [128, 4, 3, 128], U32)
+        fs = kt("fs", [128, 4, 3, 128], U8)
+        g0r = kt("g0r", [128, 4, 1152], BF16)
+        xhat = kt("xhat", [128, 4, R], F32)
+        dc = kt("dc", [128, 4, R], BF16)
+        gB = kt("gB", [128, R], F32)
+        c2 = kt("c2", [128, 4, 32, 2], BF16)
+        s2 = kt("s2", [128, 4, 32, 2], BF16)
+        sums = kt("sums", [128, 4, 2], F32)
+
+        for e in range(2):
+            nc.gpsimd.tensor_copy(out=c2[:, :, :, e], in_=cosb[:])
+        nc.gpsimd.tensor_scalar(out=s2[:, :, :, 0], in0=sinb[:], scalar1=-1.0, scalar2=0.0, op0=MULT, op1=ADD)
+        nc.gpsimd.tensor_copy(out=s2[:, :, :, 1], in_=sinb[:])
+        c2f = c2[:].rearrange("p j w e -> p j (w e)")
+        s2f = s2[:].rearrange("p j w e -> p j (w e)")
+
+        def rotate(seg, j, n):
+            m1 = work.tile([128, 10, 64], F32, name="m1")
+            m2 = work.tile([128, 10, 64], F32, name="m2")
+            cb = c2f[:, j, :].unsqueeze(1).to_broadcast([128, n, 64])
+            sb = s2f[:, j, :].unsqueeze(1).to_broadcast([128, n, 64])
+            nc.vector.tensor_tensor(out=m1[:, 0:n, :], in0=seg, in1=cb, op=MULT)
+            nc.vector.tensor_tensor(out=m2[:, 0:n, :], in0=seg, in1=sb, op=MULT)
+            m2s = m2[:, 0:n, :].rearrange("p s (w e) -> p (s w) e", e=2)[:, :, ::-1]
+            m1v = m1[:, 0:n, :].rearrange("p s (w e) -> p (s w) e", e=2)
+            nc.vector.tensor_tensor(
+                out=seg.rearrange("p s (w e) -> p s w e", e=2),
+                in0=m1v.rearrange("p (s w) e -> p s w e", s=n),
+                in1=m2s.rearrange("p (s w) e -> p s w e", s=n),
+                op=ADD,
+            )
+
+        def unit(srcs, codes, scales, fmt):
+            bank = ps.tile([128, 2, 2, 128], F32, name="tp", bufs=4)
+            for a in range(2):
+                for u in range(2):
+                    nc.tensor.transpose(bank[:, a, u, :], srcs[a][:, u::2], ident[:])
+            stg = stgp.tile([128, 2, 128, 4], BF16, name="stg", align_bytes=64)
+            nc.scalar.copy(out=stg[:].bitcast(F32), in_=bank[:].rearrange("p a u n -> p a n u"))
+            nc.vector.quantize_mx(out=codes.bitcast(fmt), scales=scales, in_=stg[:].rearrange("p a n t -> p (a n t)"))
+
+        count = [0]
+
+        def evac(out, in_, share=3):
+            count[0] += 1
+            if count[0] % share == 0:
+                nc.vector.tensor_copy(out=out, in_=in_)
+            else:
+                nc.scalar.copy(out=out, in_=in_)
+
+        def load_raw(src, n):
+            t = rawp.tile([128, 2048], BF16, name="raw", align_bytes=64)
+            nc.sync.dma_start(out=t[:, 0:n], in_=src)
+            return t[:].bitcast(F32), t
+
+        w2raw = {}
+
+        def load_w(pair):
+            w = wk_w if pair < 2 else wv_w
+            for a in range(2):
+                r = (pair % 2) * 2 + a
+                w2raw[(pair, a)] = load_raw(w[128 * r : 128 * r + 128, :], 2048)[0]
+
+        def do_w(pair):
+            for g in range(4):
+                srcs = [w2raw[(pair, a)][:, 256 * g : 256 * g + 256] for a in range(2)]
+                gg = g + 4 * (pair // 2)
+                c0 = 256 * (pair % 2)
+                unit(srcs, w2c[:, gg, c0 : c0 + 256], w2s[:, gg, c0 : c0 + 256], E4)
+
+        def rot_a():
+            for j in range(4):
+                seg = g0r[:, j, :].rearrange("p (s w) -> p s w", w=192)[:, :, 0:64]
+                rotate(seg, j, 6)
+
+        def tok_quant(src, n0):
+            il = work.tile([128, 512, 4], BF16, name="il", align_bytes=64)
+            nc.vector.tensor_copy(out=il[:], in_=src.rearrange("p j c -> p c j"))
+            return il
+
+        def tok_dz(src, n0):
+            il = tok_quant(src, n0)
+            nc.vector.quantize_mx(out=tcod[:, n0 : n0 + 512].bitcast(E5), scales=tsc[:, n0 : n0 + 512], in_=il[:].rearrange("p c j -> p (c j)"))
+
+        graw = {}
+
+        def load_b(j):
+            graw[(1, j)] = load_raw(g1v[:, j, :], 2048)
+            graw[(0, j)] = load_raw(g0v[:, j, 0:2048], 2048)
+
+        zc = {}
+
+        def do_b(j):
+            codes = work.tile([128, 8, 128], U32, name="zcod", align_bytes=64)
+            scales = work.tile([128, 8, 128], U8, name="zsc", align_bytes=64)
+            zc[j] = (codes, scales)
+            for half in (1, 0):
+                words, t = graw[(half, j)]
+                if half == 0:
+                    rotate(t[:, 0:1920].rearrange("p (s w) -> p s w", w=192)[:, :, 128:192], j, 10)
+                for gp in range(2):
+                    srcs = [words[:, 256 * (2 * gp + a) : 256 * (2 * gp + a) + 256] for a in range(2)]
+                    g = 4 * half + 2 * gp
+                    unit(
+                        srcs,
+                        codes[:, g : g + 2, :].rearrange("p a n -> p (a n)"),
+                        scales[:, g : g + 2, :].rearrange("p a n -> p (a n)"),
+                        E5,
+                    )
+
+        dh = {}
+
+        def mm_b(j):
+            codes, scales = zc[j]
+            acc = ps.tile([128, 512], F32, name="dh", bufs=1)
+            dh[j] = acc
+            order = (4, 5, 6, 7, 0, 1, 2, 3)
+            for i, g in enumerate(order):
+                nc.tensor.matmul_mx(
+                    out=acc[:],
+                    lhsT=codes[:, g, :].bitcast(E5),
+                    lhsT_scale=scales[:, g, :],
+                    rhs=w2c[:, g, :].bitcast(E4),
+                    rhs_scale=w2s[:, g, :],
+                    start=(i == 0),
+                    stop=(i == 7),
+                )
+
+        def ln(j):
+            e = work.tile([128, R], F32, name="e")
+            nc.vector.scalar_tensor_tensor(out=e[:], in0=dh[j][:], scalar=rt[:, j : j + 1], in1=gB[:], op0=MULT, op1=MULT, accum_out=sums[:, j, 0:1])
+            ex = work.tile([128, R], F32, name="ex")
+            nc.vector.scalar_tensor_tensor(out=ex[:], in0=e[:], scalar=1.0, in1=xhat[:, j, :], op0=MULT, op1=MULT, accum_out=sums[:, j, 1:2])
+            co = work.tile([128, 2], F32, name="co")
+            nc.vector.tensor_scalar(out=co[:], in0=sums[:, j, :], scalar1=1.0 / R, scalar2=None, op0=MULT)
+            nc.vector.tensor_scalar(out=ex[:], in0=xhat[:, j, :], scalar1=co[:, 1:2], scalar2=co[:, 0:1], op0=MULT, op1=ADD)
+            nc.vector.tensor_tensor(out=dc[:, j, :], in0=e[:], in1=ex[:], op=SUB)
+
+        xraw = {}
+
+        def load_x(h):
+            t = big.tile([128, 4, 1024], BF16, name="big", align_bytes=64)
+            nc.sync.dma_start(out=t[:], in_=xv[:, :, 1024 * h : 1024 * h + 1024])
+            xraw[h] = t
+
+        def do_x(c):
+            il = work.tile([128, 512, 4], BF16, name="il", align_bytes=64)
+            src = xraw[c // 2][:, :, 512 * (c % 2) : 512 * (c % 2) + 512]
+            nc.vector.tensor_copy(out=il[:], in_=src.rearrange("p j c -> p c j"))
+            nc.vector.quantize_mx(out=xc[:, 512 * c : 512 * c + 512].bitcast(E4), scales=xs[:, 512 * c : 512 * c + 512], in_=il[:].rearrange("p c j -> p (c j)"))
+
+        def mm_tok(out, m, n):
+            nc.tensor.matmul_mx(
+                out=out,
+                lhsT=xc[:, 128 * m : 128 * m + 128].bitcast(E4),
+                lhsT_scale=xs[:, 128 * m : 128 * m + 128],
+                rhs=tcod[:, 512 * n : 512 * n + 512].bitcast(E5),
+                rhs_scale=tsc[:, 512 * n : 512 * n + 512],
+                start=True,
+                stop=True,
+            )
+
+        def out1_rope(mp):
+            st = big.tile([128, 2, 1024], F32, name="big", align_bytes=64)
+            for a in range(2):
+                for n in range(2):
+                    acc = ps.tile([128, 512], F32, name="acc")
+                    mm_tok(acc[:], 2 * mp + a, n)
+                    evac(st[:, a, 512 * n : 512 * n + 512], acc[:])
+            nc.sync.dma_start(out=o1v[:, 2 * mp : 2 * mp + 2, 0:1024], in_=st[:])
+
+        def out1_lat(mq):
+            st = big.tile([128, 4, 512], F32, name="big", align_bytes=64)
+            for a in range(4):
+                acc = ps.tile([128, 512], F32, name="acc")
+                mm_tok(acc[:], 4 * mq + a, 2)
+                evac(st[:, a, :], acc[:], 2)
+            nc.sync.dma_start(out=o1v[:, 4 * mq : 4 * mq + 4, 1024:1536], in_=st[:])
+
+        def out0(n):
+            st = big.tile([128, 4, 512], F32, name="big", align_bytes=64)
+            for j in range(4):
+                acc = ps.tile([128, 512], F32, name="acc")
+                for g in range(3):
+                    nc.tensor.matmul_mx(
+                        out=acc[:],
+                        lhsT=fc[:, j, g, :].bitcast(E5),
+                        lhsT_scale=fs[:, j, g, :],
+                        rhs=kc[:, g, 512 * n : 512 * n + 512].bitcast(E4),
+                        rhs_scale=ks[:, g, 512 * n : 512 * n + 512],
+                        start=(g == 0),
+                        stop=(g == 2),
+                    )
+                evac(st[:, j, :], acc[:], 2)
+            nc.sync.dma_start(out=o0v[:, :, 512 * n : 512 * n + 512], in_=st[:])
+
+        kraw = {}
+
+        def load_k(n):
+            for r in range(4 * n, 4 * n + 4):
+                kraw[r] = load_raw(wkv_a_w[128 * r : 128 * r + 128, :], W)[0]
+
+        def do_k(n):
+            for rp in range(2 * n, 2 * n + 2):
+                for g in range(3):
+                    srcs = [kraw[2 * rp + a][:, 256 * g : 256 * g + 256] for a in range(2)]
+                    unit(srcs, kc[:, g, 256 * rp : 256 * rp + 256], ks[:, g, 256 * rp : 256 * rp + 256], E4)
+
+        def feat_rope(j):
+            words = g0r[:, j, :].bitcast(F32)
+            srcs = [words[:, 256 * a : 256 * a + 256] for a in range(2)]
+            unit(srcs, fc[:, j, 0:2, :].rearrange("p a n -> p (a n)"), fs[:, j, 0:2, :].rearrange("p a n -> p (a n)"), E5)
+
+        def feat_lat(j):
+            words = dc[:, j, :].bitcast(F32)
+            bank = ps.tile([128, 2, 2, 128], F32, name="tp", bufs=4)
+            for u in range(2):
+                nc.tensor.transpose(bank[:, 0, u, :], words[:, u::2], ident[:])
+            stg = stgp.tile([128, 2, 128, 4], BF16, name="stg", align_bytes=64)
+            nc.scalar.copy(out=stg[:, 0, :, :].bitcast(F32), in_=bank[:, 0, :, :].rearrange("p u n -> p n u"))
+            nc.vector.quantize_mx(out=fc[:, j, 2, :].bitcast(E5), scales=fs[:, j, 2, :], in_=stg[:, 0, :, :].rearrange("p n t -> p (n t)"))
+
+        load_w(0)
+        for h in range(2):
+            nc.sync.dma_start(out=g0r[:, 2 * h : 2 * h + 2, 0:1024], in_=g0v[:, 2 * h : 2 * h + 2, 2048:3072])
+        load_w(1)
+        do_w(0)
+        load_w(2)
+        rot_a()
+        do_w(1)
+        load_w(3)
+        load_b(0)
+        do_w(2)
+        tok_dz(g0r[:, :, 0:512], 0)
+        tok_dz(g0r[:, :, 512:1024], 512)
+        do_w(3)
+        load_x(0)
+        load_b(1)
+        do_b(0)
+        load_x(1)
+        load_b(2)
+        mm_b(0)
+        gps = ps.tile([128, 512], F32, name="acc")
+        nc.tensor.matmul(gps[:], ones[:], gz[:], start=True, stop=True)
+        nc.scalar.copy(out=gB[:], in_=gps[:])
+        nc.sync.dma_start(out=xhat[:], in_=cv)
+        load_b(3)
+        do_x(0)
+        do_x(1)
+        do_b(1)
+        for j in range(4):
+            nc.vector.tensor_scalar(out=xhat[:, j, :], in0=xhat[:, j, :], scalar1=mut[:, j : j + 1], scalar2=rt[:, j : j + 1], op0=SUB, op1=MULT)
+        ln(0)
+        mm_b(1)
+        out1_rope(0)
+        out1_rope(1)
+        do_x(2)
+        do_x(3)
+        ln(1)
+        do_b(2)
+        load_k(0)
+        mm_b(2)
+        out1_rope(2)
+        out1_rope(3)
+        ln(2)
+        do_b(3)
+        load_k(1)
+        mm_b(3)
+        out1_rope(4)
+        out1_rope(5)
+        ln(3)
+        for j in range(4):
+            feat_rope(j)
+        do_k(0)
+        out1_rope(6)
+        out1_rope(7)
+        load_k(2)
+        for j in range(4):
+            feat_lat(j)
+        tok_dz(dc[:], 1024)
+        do_k(1)
+        out0(0)
+        load_k(3)
+        out1_lat(0)
+        do_k(2)
+        out0(1)
+        out1_lat(1)
+        do_k(3)
+        out0(2)
+        out1_lat(2)
+        out0(3)
+        out1_lat(3)

@@ -16,6 +16,46 @@ SUB = mybir.AluOpType.subtract
 T, DIM, R, HN, HV, HR, W = 512, 2048, 512, 2048, 2048, 1024, 1536
 FLOPS = 2 * (T * (HN + HV) * R + 2 * T * W * DIM)
 BYTES = 2 * (T * DIM + DIM * W + R * (HN + HV) + T * (HN + HR + HV) + 256 * 64 + R) + 4 * (T * R + 2 * T) + 4 * (T * DIM + DIM * W)
+NRAW, NTP, NACC = 9, 4, 3
+FINE = (("o", 3), ("l", 3))
+LOADS = ["t","g0","w0","g1","w3","w2","w1","b0","w4","w5","a1","s","w7","a0","w6","b1","k0","x0","b2","a3","a2","k1","c","b3","x1","k6","k3","k2","k4","k7","k10","k5","k9","k8","k13","k11","k12","k15","k14"]
+ROWS = [
+    (["W 1 2","W 1 3"], ["tab","ra 0","ra 1","ra 3","ra 2"], []),
+    (["W 1 0","W 1 1"], [], []),
+    (["W 0 0","W 0 1"], ["rb 0"], []),
+    (["W 0 2","W 0 3"], [], []),
+    (["W 2 0","W 2 1"], ["ti 0"], []),
+    (["Z 0 1 0","Z 0 1 1"], ["ti 1"], []),
+    (["W 2 2","W 2 3"], ["tq 0","tq 1"], []),
+    (["Z 1 1 0","Z 1 1 1"], [], []),
+    (["W 3 0","W 3 1"], ["rb 1"], []),
+    (["Z 0 0 0","Z 0 0 1"], [], ["gb S"]),
+    (["W 3 2","W 3 3"], ["xi 0 S"], []),
+    (["Z 1 0 0","Z 1 0 1"], ["xi 1 S","rb 2","la 0"], ["dh 0 0 8"]),
+    (["Z 2 1 0","Z 2 1 1"], ["xq 0","xh 0","lb 0","xh 1","xq 1","rb 3"], []),
+    (["K 0 0","K 0 1"], ["lc 0","xi 2","la 1","xh 2"], ["A 2 S S","dh 1 0 8","A 1 S S","A 5 S V","A 7 S S","A 3 S S"]),
+    (["Z 2 0 0","Z 2 0 1"], ["ld 0"], ["A 6 S V"]),
+    (["Z 3 0 0","Z 3 0 1"], [], ["A 4 S V"]),
+    (["F 0","F 1"], ["xi 3","xq 2","xq 3"], []),
+    (["Z 3 1 0","Z 3 1 1"], ["la 2","lb 1"], ["A 0 S S","dh 2 0 8","A 13 S V"]),
+    (["K 0 2","K 1 0"], ["lc 1","lb 2","ld 1","xh 3","la 3"], ["A 9 S S","dh 3 0 8","A 12 S S"]),
+    (["K 3 1","K 3 2"], ["lb 3","lc 2","lc 3"], ["A 8 S V"]),
+    (["K 2 2","K 3 0"], ["ld 2"], ["A 11 S V"]),
+    (["K 2 0","K 2 1"], [], []),
+    (["K 1 1","K 1 2"], ["ld 3","ti 2"], []),
+    (["F 2","F 3"], ["tq 2"], ["A 15 S V"]),
+    (["D 0","D 1"], [], ["A 10 S S"]),
+    ([], [], []),
+    (["K 5 1","K 5 2"], [], ["l 1 S","A 14 V S"]),
+    (["K 4 2","K 5 0"], [], ["o 1 2 S","l 0 V","o 0 1 V","l 3 S","o 0 3 S","l 2 S","l 11 S"]),
+    (["K 4 0","K 4 1"], [], ["o 0 2 S","l 5 V","o 0 0 S","o 1 1 V","o 1 0 S","l 7 V","l 9 V","l 6 V"]),
+    ([], [], ["o 1 3 V"]),
+    (["K 6 2","K 7 0"], [], ["l 12 S","l 8 S","l 10 V"]),
+    (["K 6 0","K 6 1"], [], []),
+    (["K 7 1","K 7 2"], [], ["l 13 V","l 4 V","o 2 2 S","o 2 1 V"]),
+    ([], [], ["o 2 3 V","o 2 0 V","o 3 0 S","o 3 1 S","l 14 S","l 15 S","o 3 2 V","o 3 3 V"]),
+    ([], [], []),
+]
 
 
 def tile_mla_pa_v_kernel(
@@ -35,7 +75,7 @@ def tile_mla_pa_v_kernel(
 
     with ExitStack() as ctx:
         keep = ctx.enter_context(tc.tile_pool(name="keep", bufs=1))
-        rawp = ctx.enter_context(tc.tile_pool(name="rawp", bufs=10))
+        rawp = ctx.enter_context(tc.tile_pool(name="rawp", bufs=NRAW))
         big = ctx.enter_context(tc.tile_pool(name="big", bufs=5))
         stgp = ctx.enter_context(tc.tile_pool(name="stgp", bufs=6))
         work = ctx.enter_context(tc.tile_pool(name="work", bufs=2))
@@ -52,15 +92,8 @@ def tile_mla_pa_v_kernel(
         nc.gpsimd.memset(gz[:], 0.0)
         cosb = kt("cosb", [128, 4, 32], BF16)
         sinb = kt("sinb", [128, 4, 32], BF16)
-        for h in range(2):
-            nc.scalar.dma_start(out=cosb[64 * h : 64 * h + 64], in_=cosv)
-            nc.scalar.dma_start(out=sinb[64 * h : 64 * h + 64], in_=sinv)
         mut = kt("mut", [128, 4], F32)
         rt = kt("rt", [128, 4], F32)
-        nc.scalar.dma_start(out=mut[:], in_=muv)
-        nc.scalar.dma_start(out=rt[:], in_=rv)
-        nc.scalar.dma_start(out=gz[0:1, :], in_=kvn_g.rearrange("(o w) -> o w", o=1))
-
         w2c = kt("w2c", [128, 8, R], U32)
         w2s = kt("w2s", [128, 8, R], U8)
         xc = kt("xc", [128, DIM], U32)
@@ -78,287 +111,271 @@ def tile_mla_pa_v_kernel(
         c2 = kt("c2", [128, 4, 32, 2], BF16)
         s2 = kt("s2", [128, 4, 32, 2], BF16)
         sums = kt("sums", [128, 4, 2], F32)
-
-        for e in range(2):
-            nc.gpsimd.tensor_copy(out=c2[:, :, :, e], in_=cosb[:])
-        nc.gpsimd.tensor_scalar(out=s2[:, :, :, 0], in0=sinb[:], scalar1=-1.0, scalar2=0.0, op0=MULT, op1=ADD)
-        nc.gpsimd.tensor_copy(out=s2[:, :, :, 1], in_=sinb[:])
         c2f = c2[:].rearrange("p j w e -> p j (w e)")
         s2f = s2[:].rearrange("p j w e -> p j (w e)")
 
+        def tab():
+            for e in range(2):
+                nc.vector.tensor_copy(out=c2[:, :, :, e], in_=cosb[:])
+            nc.vector.tensor_scalar(out=s2[:, :, :, 0], in0=sinb[:], scalar1=-1.0, scalar2=None, op0=MULT)
+            nc.vector.tensor_copy(out=s2[:, :, :, 1], in_=sinb[:])
+
         def rotate(seg, j, n):
-            m1 = work.tile([128, 10, 64], F32, name="m1")
-            m2 = work.tile([128, 10, 64], F32, name="m2")
             cb = c2f[:, j, :].unsqueeze(1).to_broadcast([128, n, 64])
             sb = s2f[:, j, :].unsqueeze(1).to_broadcast([128, n, 64])
+            m1 = work.tile([128, 10, 64], F32, name="m1", bufs=1)
             nc.vector.tensor_tensor(out=m1[:, 0:n, :], in0=seg, in1=cb, op=MULT)
+            m2 = work.tile([128, 10, 64], F32, name="m2", bufs=1)
             nc.vector.tensor_tensor(out=m2[:, 0:n, :], in0=seg, in1=sb, op=MULT)
-            m2s = m2[:, 0:n, :].rearrange("p s (w e) -> p (s w) e", e=2)[:, :, ::-1]
-            m1v = m1[:, 0:n, :].rearrange("p s (w e) -> p (s w) e", e=2)
             nc.vector.tensor_tensor(
                 out=seg.rearrange("p s (w e) -> p s w e", e=2),
-                in0=m1v.rearrange("p (s w) e -> p s w e", s=n),
-                in1=m2s.rearrange("p (s w) e -> p s w e", s=n),
+                in0=m1[:, 0:n, :].rearrange("p s (w e) -> p s w e", e=2),
+                in1=m2[:, 0:n, :].rearrange("p s (w e) -> p s w e", e=2)[:, :, :, ::-1],
                 op=ADD,
             )
 
-        def unit(srcs, codes, scales, fmt):
-            bank = ps.tile([128, 2, 2, 128], F32, name="tp", bufs=4)
-            for a in range(2):
-                for u in range(2):
-                    nc.tensor.transpose(bank[:, a, u, :], srcs[a][:, u::2], ident[:])
-            stg = stgp.tile([128, 2, 128, 4], BF16, name="stg", align_bytes=64)
-            nc.scalar.copy(out=stg[:].bitcast(F32), in_=bank[:].rearrange("p a u n -> p a n u"))
-            nc.vector.quantize_mx(out=codes.bitcast(fmt), scales=scales, in_=stg[:].rearrange("p a n t -> p (a n t)"))
-
-        count = [0]
-
-        def evac(out, in_, share=3):
-            count[0] += 1
-            if count[0] % share == 0:
+        def put(eng, out, in_):
+            if eng == "V":
                 nc.vector.tensor_copy(out=out, in_=in_)
             else:
                 nc.scalar.copy(out=out, in_=in_)
 
-        def load_raw(src, n):
+        raw = {}
+
+        def load_raw(key, src, n, parts=1):
             t = rawp.tile([128, 2048], BF16, name="raw", align_bytes=64)
-            nc.sync.dma_start(out=t[:, 0:n], in_=src)
-            return t[:].bitcast(F32), t
-
-        w2raw = {}
-
-        def load_w(pair):
-            w = wk_w if pair < 2 else wv_w
-            for a in range(2):
-                r = (pair % 2) * 2 + a
-                w2raw[(pair, a)] = load_raw(w[128 * r : 128 * r + 128, :], 2048)[0]
-
-        def do_w(pair):
-            for g in range(4):
-                srcs = [w2raw[(pair, a)][:, 256 * g : 256 * g + 256] for a in range(2)]
-                gg = g + 4 * (pair // 2)
-                c0 = 256 * (pair % 2)
-                unit(srcs, w2c[:, gg, c0 : c0 + 256], w2s[:, gg, c0 : c0 + 256], E4)
-
-        def rot_a():
-            for j in range(4):
-                seg = g0r[:, j, :].rearrange("p (s w) -> p s w", w=192)[:, :, 0:64]
-                rotate(seg, j, 6)
-
-        def tok_quant(src, n0):
-            il = work.tile([128, 512, 4], BF16, name="il", align_bytes=64)
-            nc.vector.tensor_copy(out=il[:], in_=src.rearrange("p j c -> p c j"))
-            return il
-
-        def tok_dz(src, n0):
-            il = tok_quant(src, n0)
-            nc.vector.quantize_mx(out=tcod[:, n0 : n0 + 512].bitcast(E5), scales=tsc[:, n0 : n0 + 512], in_=il[:].rearrange("p c j -> p (c j)"))
-
-        graw = {}
-
-        def load_b(j):
-            graw[(1, j)] = load_raw(g1v[:, j, :], 2048)
-            graw[(0, j)] = load_raw(g0v[:, j, 0:2048], 2048)
-
-        zc = {}
-
-        def do_b(j):
-            codes = work.tile([128, 8, 128], U32, name="zcod", align_bytes=64)
-            scales = work.tile([128, 8, 128], U8, name="zsc", align_bytes=64)
-            zc[j] = (codes, scales)
-            for half in (1, 0):
-                words, t = graw[(half, j)]
-                if half == 0:
-                    rotate(t[:, 0:1920].rearrange("p (s w) -> p s w", w=192)[:, :, 128:192], j, 10)
-                for gp in range(2):
-                    srcs = [words[:, 256 * (2 * gp + a) : 256 * (2 * gp + a) + 256] for a in range(2)]
-                    g = 4 * half + 2 * gp
-                    unit(
-                        srcs,
-                        codes[:, g : g + 2, :].rearrange("p a n -> p (a n)"),
-                        scales[:, g : g + 2, :].rearrange("p a n -> p (a n)"),
-                        E5,
-                    )
-
-        dh = {}
-
-        def mm_b(j):
-            codes, scales = zc[j]
-            acc = ps.tile([128, 512], F32, name="dh", bufs=1)
-            dh[j] = acc
-            order = (4, 5, 6, 7, 0, 1, 2, 3)
-            for i, g in enumerate(order):
-                nc.tensor.matmul_mx(
-                    out=acc[:],
-                    lhsT=codes[:, g, :].bitcast(E5),
-                    lhsT_scale=scales[:, g, :],
-                    rhs=w2c[:, g, :].bitcast(E4),
-                    rhs_scale=w2s[:, g, :],
-                    start=(i == 0),
-                    stop=(i == 7),
-                )
-
-        def ln(j):
-            e = work.tile([128, R], F32, name="e")
-            nc.vector.scalar_tensor_tensor(out=e[:], in0=dh[j][:], scalar=rt[:, j : j + 1], in1=gB[:], op0=MULT, op1=MULT, accum_out=sums[:, j, 0:1])
-            ex = work.tile([128, R], F32, name="ex")
-            nc.vector.scalar_tensor_tensor(out=ex[:], in0=e[:], scalar=1.0, in1=xhat[:, j, :], op0=MULT, op1=MULT, accum_out=sums[:, j, 1:2])
-            co = work.tile([128, 2], F32, name="co")
-            nc.vector.tensor_scalar(out=co[:], in0=sums[:, j, :], scalar1=1.0 / R, scalar2=None, op0=MULT)
-            nc.vector.tensor_scalar(out=ex[:], in0=xhat[:, j, :], scalar1=co[:, 1:2], scalar2=co[:, 0:1], op0=MULT, op1=ADD)
-            nc.vector.tensor_tensor(out=dc[:, j, :], in0=e[:], in1=ex[:], op=SUB)
+            for i in range(parts):
+                nc.sync.dma_start(out=t[:, i * n // parts : (i + 1) * n // parts], in_=src[:, i * n // parts : (i + 1) * n // parts])
+            raw[key] = t
 
         xraw = {}
 
-        def load_x(h):
-            t = big.tile([128, 4, 1024], BF16, name="big", align_bytes=64)
-            nc.sync.dma_start(out=t[:], in_=xv[:, :, 1024 * h : 1024 * h + 1024])
-            xraw[h] = t
+        def load(name):
+            k = name[0]
+            i = int(name[1:] or 0)
+            if k == "w":
+                w = wk_w if i < 4 else wv_w
+                load_raw(name, w[128 * (i % 4) : 128 * (i % 4) + 128, :], 2048, 2 if i < 2 else 1)
+            elif k == "a":
+                load_raw(name, g1v[:, i, :], 2048)
+            elif k == "b":
+                load_raw(name, g0v[:, i, 0:2048], 2048)
+            elif k == "k":
+                load_raw(name, wkv_a_w[128 * i : 128 * i + 128, :], W)
+            elif k == "x":
+                t = big.tile([128, 4, 1024], BF16, name="big", align_bytes=64)
+                nc.sync.dma_start(out=t[:], in_=xv[:, :, 1024 * i : 1024 * i + 1024])
+                xraw[i] = t
+            elif k == "g":
+                nc.sync.dma_start(out=g0r[:, 2 * i : 2 * i + 2, 0:1024], in_=g0v[:, 2 * i : 2 * i + 2, 2048:3072])
+            elif k == "c":
+                nc.sync.dma_start(out=xhat[:], in_=cv)
+            elif k == "t":
+                for h in range(2):
+                    nc.sync.dma_start(out=cosb[64 * h : 64 * h + 64], in_=cosv)
+                    nc.sync.dma_start(out=sinb[64 * h : 64 * h + 64], in_=sinv)
+            elif k == "s":
+                nc.sync.dma_start(out=mut[:], in_=muv)
+                nc.sync.dma_start(out=rt[:], in_=rv)
+                nc.sync.dma_start(out=gz[0:1, :], in_=kvn_g.rearrange("(o w) -> o w", o=1))
 
-        def do_x(c):
-            il = work.tile([128, 512, 4], BF16, name="il", align_bytes=64)
-            src = xraw[c // 2][:, :, 512 * (c % 2) : 512 * (c % 2) + 512]
-            nc.vector.tensor_copy(out=il[:], in_=src.rearrange("p j c -> p c j"))
-            nc.vector.quantize_mx(out=xc[:, 512 * c : 512 * c + 512].bitcast(E4), scales=xs[:, 512 * c : 512 * c + 512], in_=il[:].rearrange("p c j -> p (c j)"))
+        zc = {}
 
-        def mm_tok(out, m, n):
-            nc.tensor.matmul_mx(
-                out=out,
-                lhsT=xc[:, 128 * m : 128 * m + 128].bitcast(E4),
-                lhsT_scale=xs[:, 128 * m : 128 * m + 128],
-                rhs=tcod[:, 512 * n : 512 * n + 512].bitcast(E5),
-                rhs_scale=tsc[:, 512 * n : 512 * n + 512],
-                start=True,
-                stop=True,
-            )
+        def rw(key, g):
+            return raw[key][:].bitcast(F32)[:, 256 * g : 256 * g + 256]
 
-        def out1_rope(mp):
-            st = big.tile([128, 2, 1024], F32, name="big", align_bytes=64)
+        def unit_keys(name):
+            k, *a = name.split()
+            a = [int(z) for z in a]
+            if k in "WK":
+                return [("w%d" if k == "W" else "k%d") % (2 * a[0] + i) for i in range(2)]
+            return [("a%d" if a[1] else "b%d") % a[0]] if k == "Z" else []
+
+        def unit(name):
+            k, *a = name.split()
+            a = [int(z) for z in a]
+            if k == "W":
+                pair, g = a
+                gg, c0 = g + 4 * (pair // 2), 256 * (pair % 2)
+                return [rw("w%d" % (2 * pair + i), g) for i in range(2)], (lambda: (w2c[:, gg, c0 : c0 + 256], w2s[:, gg, c0 : c0 + 256])), E4
+            if k == "Z":
+                j, half, gp = a
+                g = 4 * half + 2 * gp
+
+                def dst():
+                    if j not in zc:
+                        codes = work.tile([128, 8, 128], U32, name="zcod", align_bytes=64)
+                        scales = work.tile([128, 8, 128], U8, name="zsc", align_bytes=64)
+                        zc[j] = (codes, scales)
+                    return [t[:, g : g + 2, :].rearrange("p a n -> p (a n)") for t in zc[j]]
+
+                return [rw(("a%d" if half else "b%d") % j, 2 * gp + i) for i in range(2)], dst, E5
+            if k == "K":
+                rp, g = a
+                return [rw("k%d" % (2 * rp + i), g) for i in range(2)], (lambda: (kc[:, g, 256 * rp : 256 * rp + 256], ks[:, g, 256 * rp : 256 * rp + 256])), E4
+            if k == "F":
+                j = a[0]
+                wd = g0r[:, j, :].bitcast(F32)
+                return [wd[:, 256 * i : 256 * i + 256] for i in range(2)], (lambda: [t[:, j, 0:2, :].rearrange("p a n -> p (a n)") for t in (fc, fs)]), E5
+            if k == "D":
+                jp = a[0]
+                return [dc[:, 2 * jp + i, :].bitcast(F32) for i in range(2)], (lambda: [t[:, 2 * jp : 2 * jp + 2, 2, :] for t in (fc, fs)]), E5
+
+        def transposes(name):
+            src, dst, fmt = unit(name)
+            bank = ps.tile([128, 2, 2, 128], F32, name="tp", bufs=NTP)
             for a in range(2):
-                for n in range(2):
-                    acc = ps.tile([128, 512], F32, name="acc")
-                    mm_tok(acc[:], 2 * mp + a, n)
-                    evac(st[:, a, 512 * n : 512 * n + 512], acc[:])
-            nc.sync.dma_start(out=o1v[:, 2 * mp : 2 * mp + 2, 0:1024], in_=st[:])
+                for u in range(2):
+                    nc.tensor.transpose(bank[:, a, u, :], src[a][:, u::2], ident[:])
+            return [bank, dst, fmt, None]
 
-        def out1_lat(mq):
-            st = big.tile([128, 4, 512], F32, name="big", align_bytes=64)
-            for a in range(4):
-                acc = ps.tile([128, 512], F32, name="acc")
-                mm_tok(acc[:], 4 * mq + a, 2)
-                evac(st[:, a, :], acc[:], 2)
-            nc.sync.dma_start(out=o1v[:, 4 * mq : 4 * mq + 4, 1024:1536], in_=st[:])
-
-        def out0(n):
-            st = big.tile([128, 4, 512], F32, name="big", align_bytes=64)
-            for j in range(4):
-                acc = ps.tile([128, 512], F32, name="acc")
-                for g in range(3):
-                    nc.tensor.matmul_mx(
-                        out=acc[:],
-                        lhsT=fc[:, j, g, :].bitcast(E5),
-                        lhsT_scale=fs[:, j, g, :],
-                        rhs=kc[:, g, 512 * n : 512 * n + 512].bitcast(E4),
-                        rhs_scale=ks[:, g, 512 * n : 512 * n + 512],
-                        start=(g == 0),
-                        stop=(g == 2),
-                    )
-                evac(st[:, j, :], acc[:], 2)
-            nc.sync.dma_start(out=o0v[:, :, 512 * n : 512 * n + 512], in_=st[:])
-
-        kraw = {}
-
-        def load_k(n):
-            for r in range(4 * n, 4 * n + 4):
-                kraw[r] = load_raw(wkv_a_w[128 * r : 128 * r + 128, :], W)[0]
-
-        def do_k(n):
-            for rp in range(2 * n, 2 * n + 2):
-                for g in range(3):
-                    srcs = [kraw[2 * rp + a][:, 256 * g : 256 * g + 256] for a in range(2)]
-                    unit(srcs, kc[:, g, 256 * rp : 256 * rp + 256], ks[:, g, 256 * rp : 256 * rp + 256], E4)
-
-        def feat_rope(j):
-            words = g0r[:, j, :].bitcast(F32)
-            srcs = [words[:, 256 * a : 256 * a + 256] for a in range(2)]
-            unit(srcs, fc[:, j, 0:2, :].rearrange("p a n -> p (a n)"), fs[:, j, 0:2, :].rearrange("p a n -> p (a n)"), E5)
-
-        def feat_lat(j):
-            words = dc[:, j, :].bitcast(F32)
-            bank = ps.tile([128, 2, 2, 128], F32, name="tp", bufs=4)
-            for u in range(2):
-                nc.tensor.transpose(bank[:, 0, u, :], words[:, u::2], ident[:])
+        def empty(h, eng):
             stg = stgp.tile([128, 2, 128, 4], BF16, name="stg", align_bytes=64)
-            nc.scalar.copy(out=stg[:, 0, :, :].bitcast(F32), in_=bank[:, 0, :, :].rearrange("p u n -> p n u"))
-            nc.vector.quantize_mx(out=fc[:, j, 2, :].bitcast(E5), scales=fs[:, j, 2, :], in_=stg[:, 0, :, :].rearrange("p n t -> p (n t)"))
+            put(eng, stg[:].bitcast(F32), h[0][:].rearrange("p a u n -> p a n u"))
+            h[3] = stg
 
-        load_w(0)
-        for h in range(2):
-            nc.sync.dma_start(out=g0r[:, 2 * h : 2 * h + 2, 0:1024], in_=g0v[:, 2 * h : 2 * h + 2, 2048:3072])
-        load_w(1)
-        do_w(0)
-        load_w(2)
-        rot_a()
-        do_w(1)
-        load_w(3)
-        load_b(0)
-        do_w(2)
-        tok_dz(g0r[:, :, 0:512], 0)
-        tok_dz(g0r[:, :, 512:1024], 512)
-        do_w(3)
-        load_x(0)
-        load_b(1)
-        do_b(0)
-        load_x(1)
-        load_b(2)
-        mm_b(0)
-        gps = ps.tile([128, 512], F32, name="acc")
-        nc.tensor.matmul(gps[:], ones[:], gz[:], start=True, stop=True)
-        nc.scalar.copy(out=gB[:], in_=gps[:])
-        nc.sync.dma_start(out=xhat[:], in_=cv)
-        load_b(3)
-        do_x(0)
-        do_x(1)
-        do_b(1)
-        for j in range(4):
-            nc.vector.tensor_scalar(out=xhat[:, j, :], in0=xhat[:, j, :], scalar1=mut[:, j : j + 1], scalar2=rt[:, j : j + 1], op0=SUB, op1=MULT)
-        ln(0)
-        mm_b(1)
-        out1_rope(0)
-        out1_rope(1)
-        do_x(2)
-        do_x(3)
-        ln(1)
-        do_b(2)
-        load_k(0)
-        mm_b(2)
-        out1_rope(2)
-        out1_rope(3)
-        ln(2)
-        do_b(3)
-        load_k(1)
-        mm_b(3)
-        out1_rope(4)
-        out1_rope(5)
-        ln(3)
-        for j in range(4):
-            feat_rope(j)
-        do_k(0)
-        out1_rope(6)
-        out1_rope(7)
-        load_k(2)
-        for j in range(4):
-            feat_lat(j)
-        tok_dz(dc[:], 1024)
-        do_k(1)
-        out0(0)
-        load_k(3)
-        out1_lat(0)
-        do_k(2)
-        out0(1)
-        out1_lat(1)
-        do_k(3)
-        out0(2)
-        out1_lat(2)
-        out0(3)
-        out1_lat(3)
+        def quantize(h):
+            codes, scales = h[1]()
+            stg = h[3]
+            if len(codes.shape) == 3:
+                for a in range(2):
+                    nc.vector.quantize_mx(out=codes[:, a, :].bitcast(h[2]), scales=scales[:, a, :], in_=stg[:, a, :, :].rearrange("p n t -> p (n t)"))
+            else:
+                nc.vector.quantize_mx(out=codes.bitcast(h[2]), scales=scales, in_=stg[:].rearrange("p a n t -> p (a n t)"))
+
+        ils, lt, ex = {}, {}, {}
+
+        def vtask(name, dh):
+            k, *a = name.split()
+            i = int(a[0]) if a else 0
+            if k == "tab":
+                tab()
+            elif k == "ra":
+                rotate(g0r[:, i, :].rearrange("p (s w) -> p s w", w=192)[:, :, 0:64], i, 6)
+            elif k == "rb":
+                rotate(raw["b%d" % i][:, 0:1920].rearrange("p (s w) -> p s w", w=192)[:, :, 128:192], i, 10)
+            elif k in ("xi", "ti"):
+                il = work.tile([128, 512, 4], BF16, name="il", align_bytes=64)
+                if k == "xi":
+                    src = xraw[i // 2][:, :, 512 * (i % 2) : 512 * (i % 2) + 512]
+                elif i < 2:
+                    src = g0r[:, :, 512 * i : 512 * i + 512]
+                else:
+                    src = dc[:]
+                put(a[1] if len(a) > 1 else "V", il[:], src.rearrange("p j c -> p c j"))
+                ils[(k[0], i)] = il
+            elif k in ("xq", "tq"):
+                codes, scales, fmt = (xc, xs, E4) if k == "xq" else (tcod, tsc, E5)
+                nc.vector.quantize_mx(out=codes[:, 512 * i : 512 * i + 512].bitcast(fmt), scales=scales[:, 512 * i : 512 * i + 512], in_=ils[(k[0], i)][:].rearrange("p c j -> p (c j)"))
+            elif k == "xh":
+                nc.vector.tensor_scalar(out=xhat[:, i, :], in0=xhat[:, i, :], scalar1=mut[:, i : i + 1], scalar2=rt[:, i : i + 1], op0=SUB, op1=MULT)
+            elif k == "la":
+                lt[i] = e = work.tile([128, R], F32, name="e")
+                nc.vector.scalar_tensor_tensor(out=e[:], in0=dh[i][:], scalar=rt[:, i : i + 1], in1=gB[:], op0=MULT, op1=MULT, accum_out=sums[:, i, 0:1])
+            elif k == "lb":
+                ex[i] = z = work.tile([128, R], F32, name="ex")
+                nc.vector.scalar_tensor_tensor(out=z[:], in0=lt[i][:], scalar=1.0, in1=xhat[:, i, :], op0=MULT, op1=MULT, accum_out=sums[:, i, 1:2])
+            elif k == "lc":
+                nc.vector.tensor_scalar(out=sums[:, i, :], in0=sums[:, i, :], scalar1=1.0 / R, scalar2=None, op0=MULT)
+                nc.vector.tensor_scalar(out=ex[i][:], in0=xhat[:, i, :], scalar1=sums[:, i, 1:2], scalar2=sums[:, i, 0:1], op0=MULT, op1=ADD)
+            elif k == "ld":
+                nc.vector.tensor_tensor(out=dc[:, i, :], in0=lt[i][:], in1=ex[i][:], op=SUB)
+            else:
+                assert 0, name
+
+        dh, stage = {}, {}
+
+        def mm(acc, l, ls, r, rs, fl, fr, start, stop):
+            nc.tensor.matmul_mx(out=acc, lhsT=l.bitcast(fl), lhsT_scale=ls, rhs=r.bitcast(fr), rhs_scale=rs, start=start, stop=stop)
+
+        pend = []
+
+        def bank():
+            if len(pend) == NACC:
+                drain(*pend.pop(0))
+            t = ps.tile([128, 512], F32, name="acc", bufs=NACC)
+            return t
+
+        def mtask(name):
+            k, *a = name.split()
+            eng = [z for z in a if z in "VS"]
+            a = [int(z) for z in a if z not in "VS"]
+            if k == "gb":
+                acc = bank()
+                nc.tensor.matmul(acc[:], ones[:], gz[:], start=True, stop=True)
+                pend.append((acc, None, eng[0]))
+                return
+            if k == "dh":
+                j, lo, hi = a
+                if lo == 0:
+                    acc = ps.tile([128, 512], F32, name="dh", bufs=1)
+                    dh[j] = acc
+                codes, scales = zc[j]
+                for i in range(lo, hi):
+                    mm(dh[j][:], codes[:, i, :], scales[:, i, :], w2c[:, i, :], w2s[:, i, :], E5, E4, i == 0, i == 7)
+                return
+            if k in "Al":
+                m = a[0]
+                for n in (0, 1) if k == "A" else (2,):
+                    acc = bank()
+                    mm(acc[:], xc[:, 128 * m : 128 * m + 128], xs[:, 128 * m : 128 * m + 128], tcod[:, 512 * n : 512 * n + 512], tsc[:, 512 * n : 512 * n + 512], E4, E5, True, True)
+                    pend.append((acc, (k, m, n), eng[n % 2]))
+            else:
+                n, j = a
+                acc = bank()
+                for g in range(3):
+                    mm(acc[:], fc[:, j, g, :], fs[:, j, g, :], kc[:, g, 512 * n : 512 * n + 512], ks[:, g, 512 * n : 512 * n + 512], E5, E4, g == 0, g == 2)
+                pend.append((acc, ("o", j, n), eng[0]))
+
+        def drain(acc, key, eng):
+            if key is None:
+                put(eng, gB[:], acc[:])
+                return
+            k, m, n = key
+            sk, idx = (("A", m // 2), 2 * (m % 2) + n) if k == "A" else (("l", m // 4), m % 4) if k == "l" else (("o", n), m)
+            if sk not in stage:
+                t = big.tile([128, 4, 512], F32, name="big", align_bytes=64)
+                stage[sk] = [t, 0]
+            st = stage[sk]
+            put(eng, st[0][:, idx, :], acc[:])
+            st[1] += 1
+            fine = sk in FINE
+            if st[1] == 4 or (fine and st[1] == 2):
+                lo = 2 if fine and st[1] == 4 else 0
+                hi = 2 if fine and st[1] == 2 else 4
+                i = sk[1]
+                if k == "A":
+                    nc.sync.dma_start(out=o1v[:, 2 * i : 2 * i + 2, 0:1024], in_=st[0][:].rearrange("p (m n) w -> p m (n w)", m=2))
+                elif k == "l":
+                    nc.sync.dma_start(out=o1v[:, 4 * i + lo : 4 * i + hi, 1024:1536], in_=st[0][:, lo:hi, :])
+                else:
+                    nc.sync.dma_start(out=o0v[:, lo:hi, 512 * i : 512 * i + 512], in_=st[0][:, lo:hi, :])
+
+        ctx.enter_context(tc.manual_schedule())
+        last = {}
+        for r, (run, vs, ms) in enumerate(ROWS):
+            for u in run:
+                for key in unit_keys(u):
+                    last[key] = r
+        loads, issued = list(LOADS), []
+        prev = []
+        for r, (run, vs, ms) in enumerate(ROWS):
+            while loads:
+                if loads[0][0] in "wabk":
+                    if len(issued) >= NRAW and last[issued[-NRAW]] >= r:
+                        break
+                    issued.append(loads[0])
+                load(loads.pop(0))
+            cur = [transposes(u) for u in run]
+            while pend:
+                drain(*pend.pop(0))
+            for h in prev:
+                quantize(h)
+            for h in cur:
+                empty(h, "S")
+            prev = cur
+            for m in ms:
+                mtask(m)
+            for v in vs:
+                vtask(v, dh)
+        assert not prev and not pend and not loads

@@ -16,45 +16,45 @@ SUB = mybir.AluOpType.subtract
 T, DIM, R, HN, HV, HR, W = 512, 2048, 512, 2048, 2048, 1024, 1536
 FLOPS = 2 * (T * (HN + HV) * R + 2 * T * W * DIM)
 BYTES = 2 * (T * DIM + DIM * W + R * (HN + HV) + T * (HN + HR + HV) + 256 * 64 + R) + 4 * (T * R + 2 * T) + 4 * (T * DIM + DIM * W)
-NRAW, NTP, NACC = 9, 4, 3
-FINE = (("o", 3), ("l", 3))
-LOADS = ["t","g0","w0","g1","w3","w2","w1","b0","w4","w5","a1","s","w7","a0","w6","b1","k0","x0","b2","a3","a2","k1","c","b3","x1","k6","k3","k2","k4","k7","k10","k5","k9","k8","k13","k11","k12","k15","k14"]
+NRAW, NTP, NACC, NOUT, NSTG, NKD, NZ = 10, 4, 3, 6, 3, 3, 3
+FINE = ()
+LOADS = ["g0","t","a0","g2","x1","w5","s","w4","g1","w6","w7","w0","g3","x0","w1","w2","w3","x2","a2","a3","c","k9","k6","a1","k7","x3","k10","k8","k11","k14","k5","k0","k2","k3","k13","k1","k12","k15","k4"]
 ROWS = [
-    (["W 1 2","W 1 3"], ["tab","ra 0","ra 1","ra 3","ra 2"], []),
-    (["W 1 0","W 1 1"], [], []),
-    (["W 0 0","W 0 1"], ["rb 0"], []),
-    (["W 0 2","W 0 3"], [], []),
-    (["W 2 0","W 2 1"], ["ti 0"], []),
-    (["Z 0 1 0","Z 0 1 1"], ["ti 1"], []),
-    (["W 2 2","W 2 3"], ["tq 0","tq 1"], []),
-    (["Z 1 1 0","Z 1 1 1"], [], []),
-    (["W 3 0","W 3 1"], ["rb 1"], []),
-    (["Z 0 0 0","Z 0 0 1"], [], ["gb S"]),
-    (["W 3 2","W 3 3"], ["xi 0 S"], []),
-    (["Z 1 0 0","Z 1 0 1"], ["xi 1 S","rb 2","la 0"], ["dh 0 0 8"]),
-    (["Z 2 1 0","Z 2 1 1"], ["xq 0","xh 0","lb 0","xh 1","xq 1","rb 3"], []),
-    (["K 0 0","K 0 1"], ["lc 0","xi 2","la 1","xh 2"], ["A 2 S S","dh 1 0 8","A 1 S S","A 5 S V","A 7 S S","A 3 S S"]),
-    (["Z 2 0 0","Z 2 0 1"], ["ld 0"], ["A 6 S V"]),
-    (["Z 3 0 0","Z 3 0 1"], [], ["A 4 S V"]),
-    (["F 0","F 1"], ["xi 3","xq 2","xq 3"], []),
-    (["Z 3 1 0","Z 3 1 1"], ["la 2","lb 1"], ["A 0 S S","dh 2 0 8","A 13 S V"]),
-    (["K 0 2","K 1 0"], ["lc 1","lb 2","ld 1","xh 3","la 3"], ["A 9 S S","dh 3 0 8","A 12 S S"]),
-    (["K 3 1","K 3 2"], ["lb 3","lc 2","lc 3"], ["A 8 S V"]),
-    (["K 2 2","K 3 0"], ["ld 2"], ["A 11 S V"]),
-    (["K 2 0","K 2 1"], [], []),
-    (["K 1 1","K 1 2"], ["ld 3","ti 2"], []),
-    (["F 2","F 3"], ["tq 2"], ["A 15 S V"]),
-    (["D 0","D 1"], [], ["A 10 S S"]),
-    ([], [], []),
-    (["K 5 1","K 5 2"], [], ["l 1 S","A 14 V S"]),
-    (["K 4 2","K 5 0"], [], ["o 1 2 S","l 0 V","o 0 1 V","l 3 S","o 0 3 S","l 2 S","l 11 S"]),
-    (["K 4 0","K 4 1"], [], ["o 0 2 S","l 5 V","o 0 0 S","o 1 1 V","o 1 0 S","l 7 V","l 9 V","l 6 V"]),
-    ([], [], ["o 1 3 V"]),
-    (["K 6 2","K 7 0"], [], ["l 12 S","l 8 S","l 10 V"]),
-    (["K 6 0","K 6 1"], [], []),
-    (["K 7 1","K 7 2"], [], ["l 13 V","l 4 V","o 2 2 S","o 2 1 V"]),
-    ([], [], ["o 2 3 V","o 2 0 V","o 3 0 S","o 3 1 S","l 14 S","l 15 S","o 3 2 V","o 3 3 V"]),
-    ([], [], []),
+    ("", "VV", ["tab","ra 0","rc 0"], []),
+    ("Z 0 1", "SS", ["xi 1 S","ra 2","rc 2"], []),
+    ("Z 0 0", "SS", ["ra 1"], []),
+    ("Z 2 0", "SS", ["rc 1"], []),
+    ("W 5", "SS", [], []),
+    ("W 6", "SS", [], []),
+    ("W 4", "SS", ["xq 1"], []),
+    ("W 7", "SS", [], []),
+    ("F 0", "SS", ["ra 3"], []),
+    ("Z 1 0", "SS", [], ["gb S"]),
+    ("W 2", "SS", [], []),
+    ("W 0", "SS", ["rc 3"], []),
+    ("W 1", "SS", ["xi 0 V"], []),
+    ("W 3", "SS", ["xh 0"], []),
+    ("Z 2 1", "SS", ["xh 1"], []),
+    ("Z 3 1", "SS", ["d 9 V","xh 2","la 0","xi 2 S","xq 0","xq 2","d 7 S"], ["dh 0"]),
+    ("", "VV", [], []),
+    ("Z 1 1", "SS", ["lb 0"], []),
+    ("Z 3 0", "SS", ["lc 0 V","xi 3 V","la 1","d 6 V","ti 0 S","xq 3"], ["dh 1"]),
+    ("K 2 0", "SS", [], []),
+    ("K 2 1", "SS", ["ld 0","xh 3","ti 1 S","la 2","lb 1","tq 0","lc 1 S","tq 1"], ["dh 2"]),
+    ("K 2 2", "SS", ["la 3","d 5 S","lb 2","lb 3","ld 1","lc 2 V"], ["dh 3"]),
+    ("K 0 1", "SS", ["lc 3 V"], ["A 8 S S","A 4 S S","A 6 V S"]),
+    ("K 1 1", "SV", [], ["A 9 V S","A 11 V S"]),
+    ("F 1", "SS", ["ld 2","ld 3"], ["A 1 V S","A 3 S S"]),
+    ("K 0 2", "SV", [], ["A 10 S S","A 13 V V"]),
+    ("D", "SS", [], ["A 12 V S","A 14 S S"]),
+    ("K 0 0", "SS", ["ti 2 V"], ["A 15 S V"]),
+    ("K 3 0", "SS", ["tq 2"], ["A 7 V S"]),
+    ("K 3 1", "SV", [], ["l 9 V","l 8 S","A 5 S V"]),
+    ("K 1 0", "SS", [], ["A 0 S V","l 5 S","l 4 V"]),
+    ("K 3 2", "SV", [], []),
+    ("K 1 2", "SV", [], ["l 12 S"]),
+    ("", "VS", [], ["l 13 S","A 2 S S","o 0 1 V","o 0 2 S","l 0 V","l 1 S","o 1 1 S","l 15 V","o 1 2 S","l 7 V","o 3 0 S","l 14 V","l 6 V","o 2 0 S","o 1 3 S","o 0 3 V","l 11 V","l 3 V","l 2 V","o 2 3 V","o 3 2 S","o 2 2 S","l 10 S","o 1 0 S","o 3 3 S","o 0 0 V","o 2 1 S","o 3 1 V"]),
+    ("", "VS", [], []),
 ]
 
 
@@ -76,8 +76,8 @@ def tile_mla_pa_v_kernel(
     with ExitStack() as ctx:
         keep = ctx.enter_context(tc.tile_pool(name="keep", bufs=1))
         rawp = ctx.enter_context(tc.tile_pool(name="rawp", bufs=NRAW))
-        big = ctx.enter_context(tc.tile_pool(name="big", bufs=5))
-        stgp = ctx.enter_context(tc.tile_pool(name="stgp", bufs=6))
+        outp = ctx.enter_context(tc.tile_pool(name="outp", bufs=NOUT))
+        stgp = ctx.enter_context(tc.tile_pool(name="stgp", bufs=NSTG))
         work = ctx.enter_context(tc.tile_pool(name="work", bufs=2))
         ps = ctx.enter_context(tc.psum_pool(name="ps", bufs=3))
 
@@ -94,6 +94,7 @@ def tile_mla_pa_v_kernel(
         sinb = kt("sinb", [128, 4, 32], BF16)
         mut = kt("mut", [128, 4], F32)
         rt = kt("rt", [128, 4], F32)
+        rs = kt("rs", [128, 4], F32)
         w2c = kt("w2c", [128, 8, R], U32)
         w2s = kt("w2s", [128, 8, R], U8)
         xc = kt("xc", [128, DIM], U32)
@@ -102,9 +103,11 @@ def tile_mla_pa_v_kernel(
         ks = kt("ks", [128, 3, DIM], U8)
         tcod = kt("tcod", [128, W], U32)
         tsc = kt("tsc", [128, W], U8)
-        fc = kt("fc", [128, 4, 3, 128], U32)
-        fs = kt("fs", [128, 4, 3, 128], U8)
-        g0r = kt("g0r", [128, 4, 1152], BF16)
+        fc = kt("fc", [128, 4, 2, 128], U32)
+        fs = kt("fs", [128, 4, 2, 128], U8)
+        dcod = kt("dcod", [128, 4, 128], U32)
+        dsc = kt("dsc", [128, 4, 128], U8)
+        g0 = kt("g0", [128, 4, 3072], BF16)
         xhat = kt("xhat", [128, 4, R], F32)
         dc = kt("dc", [128, 4, R], BF16)
         gB = kt("gB", [128, R], F32)
@@ -114,26 +117,6 @@ def tile_mla_pa_v_kernel(
         c2f = c2[:].rearrange("p j w e -> p j (w e)")
         s2f = s2[:].rearrange("p j w e -> p j (w e)")
 
-        def tab():
-            for e in range(2):
-                nc.vector.tensor_copy(out=c2[:, :, :, e], in_=cosb[:])
-            nc.vector.tensor_scalar(out=s2[:, :, :, 0], in0=sinb[:], scalar1=-1.0, scalar2=None, op0=MULT)
-            nc.vector.tensor_copy(out=s2[:, :, :, 1], in_=sinb[:])
-
-        def rotate(seg, j, n):
-            cb = c2f[:, j, :].unsqueeze(1).to_broadcast([128, n, 64])
-            sb = s2f[:, j, :].unsqueeze(1).to_broadcast([128, n, 64])
-            m1 = work.tile([128, 10, 64], F32, name="m1", bufs=1)
-            nc.vector.tensor_tensor(out=m1[:, 0:n, :], in0=seg, in1=cb, op=MULT)
-            m2 = work.tile([128, 10, 64], F32, name="m2", bufs=1)
-            nc.vector.tensor_tensor(out=m2[:, 0:n, :], in0=seg, in1=sb, op=MULT)
-            nc.vector.tensor_tensor(
-                out=seg.rearrange("p s (w e) -> p s w e", e=2),
-                in0=m1[:, 0:n, :].rearrange("p s (w e) -> p s w e", e=2),
-                in1=m2[:, 0:n, :].rearrange("p s (w e) -> p s w e", e=2)[:, :, :, ::-1],
-                op=ADD,
-            )
-
         def put(eng, out, in_):
             if eng == "V":
                 nc.vector.tensor_copy(out=out, in_=in_)
@@ -142,32 +125,23 @@ def tile_mla_pa_v_kernel(
 
         raw = {}
 
-        def load_raw(key, src, n, parts=1):
-            t = rawp.tile([128, 2048], BF16, name="raw", align_bytes=64)
-            for i in range(parts):
-                nc.sync.dma_start(out=t[:, i * n // parts : (i + 1) * n // parts], in_=src[:, i * n // parts : (i + 1) * n // parts])
-            raw[key] = t
-
-        xraw = {}
-
         def load(name):
             k = name[0]
             i = int(name[1:] or 0)
-            if k == "w":
-                w = wk_w if i < 4 else wv_w
-                load_raw(name, w[128 * (i % 4) : 128 * (i % 4) + 128, :], 2048, 2 if i < 2 else 1)
-            elif k == "a":
-                load_raw(name, g1v[:, i, :], 2048)
-            elif k == "b":
-                load_raw(name, g0v[:, i, 0:2048], 2048)
-            elif k == "k":
-                load_raw(name, wkv_a_w[128 * i : 128 * i + 128, :], W)
-            elif k == "x":
-                t = big.tile([128, 4, 1024], BF16, name="big", align_bytes=64)
-                nc.sync.dma_start(out=t[:], in_=xv[:, :, 1024 * i : 1024 * i + 1024])
-                xraw[i] = t
+            if k in "wakx":
+                t = rawp.tile([128, 2048], BF16, name="raw", align_bytes=64)
+                raw[name] = t
+                if k == "k":
+                    nc.sync.dma_start(out=t[:, 0:W], in_=wkv_a_w[128 * i : 128 * i + 128, :])
+                elif k == "x":
+                    nc.sync.dma_start(out=t[:].rearrange("p (j c) -> p j c", j=4), in_=xv[:, :, 512 * i : 512 * i + 512])
+                elif k == "a":
+                    nc.sync.dma_start(out=t[:], in_=g1v[:, i, :])
+                else:
+                    w = wk_w if i < 4 else wv_w
+                    nc.sync.dma_start(out=t[:], in_=w[128 * (i % 4) : 128 * (i % 4) + 128, :])
             elif k == "g":
-                nc.sync.dma_start(out=g0r[:, 2 * i : 2 * i + 2, 0:1024], in_=g0v[:, 2 * i : 2 * i + 2, 2048:3072])
+                nc.sync.dma_start(out=g0[:, i, :], in_=g0v[:, i, :])
             elif k == "c":
                 nc.sync.dma_start(out=xhat[:], in_=cv)
             elif k == "t":
@@ -179,121 +153,146 @@ def tile_mla_pa_v_kernel(
                 nc.sync.dma_start(out=rt[:], in_=rv)
                 nc.sync.dma_start(out=gz[0:1, :], in_=kvn_g.rearrange("(o w) -> o w", o=1))
 
-        zc = {}
+        zc, kd = {}, {}
 
-        def rw(key, g):
-            return raw[key][:].bitcast(F32)[:, 256 * g : 256 * g + 256]
-
-        def unit_keys(name):
+        def run_keys(name):
             k, *a = name.split()
             a = [int(z) for z in a]
             if k in "WK":
-                return [("w%d" if k == "W" else "k%d") % (2 * a[0] + i) for i in range(2)]
-            return [("a%d" if a[1] else "b%d") % a[0]] if k == "Z" else []
+                return [("w%d" if k == "W" else "k%d") % (4 * (a[0] // 4 if k == "W" else a[0]) + i) for i in range(4)]
+            return ["a%d" % a[0]] if k == "Z" and a[1] else []
 
-        def unit(name):
+        def run_of(name):
             k, *a = name.split()
             a = [int(z) for z in a]
             if k == "W":
-                pair, g = a
-                gg, c0 = g + 4 * (pair // 2), 256 * (pair % 2)
-                return [rw("w%d" % (2 * pair + i), g) for i in range(2)], (lambda: (w2c[:, gg, c0 : c0 + 256], w2s[:, gg, c0 : c0 + 256])), E4
+                g = a[0]
+                return [raw[q][:].bitcast(F32)[:, 256 * (g % 4) : 256 * (g % 4) + 256] for q in run_keys(name)], (lambda: (w2c[:, g, :], w2s[:, g, :])), E4
+            if k == "K":
+                n, g = a
+                cols = slice(512 * n, 512 * n + 512)
+                return [kd[q][:, g, :, :] if q in kd else raw[q][:].bitcast(F32)[:, 256 * g : 256 * g + 256] for q in run_keys(name)], (lambda: (kc[:, g, cols], ks[:, g, cols])), E4
             if k == "Z":
-                j, half, gp = a
-                g = 4 * half + 2 * gp
+                j, half = a
 
                 def dst():
                     if j not in zc:
-                        codes = work.tile([128, 8, 128], U32, name="zcod", align_bytes=64)
-                        scales = work.tile([128, 8, 128], U8, name="zsc", align_bytes=64)
+                        codes = work.tile([128, 8, 128], U32, name="zcod", bufs=NZ, align_bytes=64)
+                        scales = work.tile([128, 8, 128], U8, name="zsc", bufs=NZ, align_bytes=64)
                         zc[j] = (codes, scales)
-                    return [t[:, g : g + 2, :].rearrange("p a n -> p (a n)") for t in zc[j]]
+                    return [t[:, 4 * half : 4 * half + 4, :].rearrange("p a n -> p (a n)") for t in zc[j]]
 
-                return [rw(("a%d" if half else "b%d") % j, 2 * gp + i) for i in range(2)], dst, E5
-            if k == "K":
-                rp, g = a
-                return [rw("k%d" % (2 * rp + i), g) for i in range(2)], (lambda: (kc[:, g, 256 * rp : 256 * rp + 256], ks[:, g, 256 * rp : 256 * rp + 256])), E4
+                wd = (raw["a%d" % j][:] if half else g0[:, j, 0:2048]).bitcast(F32)
+                return [wd[:, 256 * i : 256 * i + 256] for i in range(4)], dst, E5
             if k == "F":
-                j = a[0]
-                wd = g0r[:, j, :].bitcast(F32)
-                return [wd[:, 256 * i : 256 * i + 256] for i in range(2)], (lambda: [t[:, j, 0:2, :].rearrange("p a n -> p (a n)") for t in (fc, fs)]), E5
+                wd = [g0[:, 2 * a[0] + i, 2048:3072].bitcast(F32) for i in range(2)]
+                return [wd[i // 2][:, 256 * (i % 2) : 256 * (i % 2) + 256] for i in range(4)], (lambda: [t[:, 2 * a[0] : 2 * a[0] + 2, :, :].rearrange("p j g n -> p (j g n)") for t in (fc, fs)]), E5
             if k == "D":
-                jp = a[0]
-                return [dc[:, 2 * jp + i, :].bitcast(F32) for i in range(2)], (lambda: [t[:, 2 * jp : 2 * jp + 2, 2, :] for t in (fc, fs)]), E5
+                jj = [2 * a[0], 2 * a[0] + 1] if a else [0, 1, 2, 3]
+                return [dc[:, j, :].bitcast(F32) for j in jj], (lambda: [t[:, jj[0] : jj[-1] + 1, :].rearrange("p j n -> p (j n)") for t in (dcod, dsc)]), E5
 
         def transposes(name):
-            src, dst, fmt = unit(name)
-            bank = ps.tile([128, 2, 2, 128], F32, name="tp", bufs=NTP)
-            for a in range(2):
-                for u in range(2):
-                    nc.tensor.transpose(bank[:, a, u, :], src[a][:, u::2], ident[:])
-            return [bank, dst, fmt, None]
+            src, dst, fmt = run_of(name)
+            banks = []
+            for b in range(len(src) // 2):
+                bk = ps.tile([128, 2, 2, 128], F32, name="tp", bufs=NTP)
+                banks.append(bk)
+                for a in range(2):
+                    for u in range(2):
+                        s = src[2 * b + a]
+                        nc.tensor.transpose(bk[:, a, u, :], s[:, u, :] if len(s.shape) == 3 else s[:, u::2], ident[:])
+            return banks, dst, fmt
 
-        def empty(h, eng):
-            stg = stgp.tile([128, 2, 128, 4], BF16, name="stg", align_bytes=64)
-            put(eng, stg[:].bitcast(F32), h[0][:].rearrange("p a u n -> p a n u"))
-            h[3] = stg
+        def empty(banks, engs):
+            stg = stgp.tile([128, 4, 128, 4], BF16, name="stg", align_bytes=64)
+            for b, bk in enumerate(banks):
+                put(engs[b], stg[:, 2 * b : 2 * b + 2, :, :].bitcast(F32), bk[:].rearrange("p a u n -> p a n u"))
+            return stg
 
         def quantize(h):
-            codes, scales = h[1]()
-            stg = h[3]
-            if len(codes.shape) == 3:
-                for a in range(2):
-                    nc.vector.quantize_mx(out=codes[:, a, :].bitcast(h[2]), scales=scales[:, a, :], in_=stg[:, a, :, :].rearrange("p n t -> p (n t)"))
-            else:
-                nc.vector.quantize_mx(out=codes.bitcast(h[2]), scales=scales, in_=stg[:].rearrange("p a n t -> p (a n t)"))
+            stg, nb, dst, fmt = h
+            codes, scales = dst()
+            nc.vector.quantize_mx(out=codes.bitcast(fmt), scales=scales, in_=stg[:, 0 : 2 * nb, :, :].rearrange("p a n t -> p (a n t)"))
 
-        ils, lt, ex = {}, {}, {}
+        ils, lt, ex, rot = {}, {}, {}, {}
 
-        def vtask(name, dh):
+        def vtask(name):
             k, *a = name.split()
             i = int(a[0]) if a else 0
             if k == "tab":
-                tab()
+                for e in range(2):
+                    nc.vector.tensor_copy(out=c2[:, :, :, e], in_=cosb[:])
+                nc.vector.tensor_scalar(out=s2[:, :, :, 0], in0=sinb[:], scalar1=-1.0, scalar2=None, op0=MULT)
+                nc.vector.tensor_copy(out=s2[:, :, :, 1], in_=sinb[:])
             elif k == "ra":
-                rotate(g0r[:, i, :].rearrange("p (s w) -> p s w", w=192)[:, :, 0:64], i, 6)
-            elif k == "rb":
-                rotate(raw["b%d" % i][:, 0:1920].rearrange("p (s w) -> p s w", w=192)[:, :, 128:192], i, 10)
+                seg = g0[:, i, :].rearrange("p (h w) -> p h w", w=192)[:, :, 128:192]
+                m1 = work.tile([128, 16, 64], F32, name="m1", tag="f", bufs=3)
+                nc.vector.tensor_tensor(out=m1[:], in0=seg, in1=c2f[:, i, :].unsqueeze(1).to_broadcast([128, 16, 64]), op=MULT)
+                m2 = work.tile([128, 16, 64], F32, name="m2", tag="f", bufs=3)
+                nc.vector.tensor_tensor(out=m2[:], in0=seg, in1=s2f[:, i, :].unsqueeze(1).to_broadcast([128, 16, 64]), op=MULT)
+                rot[i] = (m1, m2)
+            elif k == "rc":
+                m1, m2 = rot[i]
+                nc.vector.tensor_tensor(
+                    out=g0[:, i, :].rearrange("p (h w) -> p h w", w=192)[:, :, 128:192].rearrange("p h (w e) -> p h w e", e=2),
+                    in0=m1[:].rearrange("p h (w e) -> p h w e", e=2),
+                    in1=m2[:].rearrange("p h (w e) -> p h w e", e=2)[:, :, :, ::-1],
+                    op=ADD,
+                )
             elif k in ("xi", "ti"):
                 il = work.tile([128, 512, 4], BF16, name="il", align_bytes=64)
                 if k == "xi":
-                    src = xraw[i // 2][:, :, 512 * (i % 2) : 512 * (i % 2) + 512]
+                    src = raw["x%d" % i][:].rearrange("p (j c) -> p j c", j=4)
                 elif i < 2:
-                    src = g0r[:, :, 512 * i : 512 * i + 512]
+                    src = g0[:, :, 2048 + 512 * i : 2560 + 512 * i]
                 else:
                     src = dc[:]
-                put(a[1] if len(a) > 1 else "V", il[:], src.rearrange("p j c -> p c j"))
+                put(a[1], il[:], src.rearrange("p j c -> p c j"))
                 ils[(k[0], i)] = il
             elif k in ("xq", "tq"):
                 codes, scales, fmt = (xc, xs, E4) if k == "xq" else (tcod, tsc, E5)
                 nc.vector.quantize_mx(out=codes[:, 512 * i : 512 * i + 512].bitcast(fmt), scales=scales[:, 512 * i : 512 * i + 512], in_=ils[(k[0], i)][:].rearrange("p c j -> p (c j)"))
+            elif k == "d":
+                t = rawp.tile([128, 3, 2, 128], F32, name="kd", bufs=NKD, align_bytes=64)
+                put(a[1], t[:], raw["k%d" % i][:].bitcast(F32)[:, 0:768].rearrange("p (g w u) -> p g u w", g=3, u=2))
+                kd["k%d" % i] = t
             elif k == "xh":
+                if i == 0:
+                    nc.vector.tensor_scalar(out=rs[:], in0=rt[:], scalar1=1.0 / R, scalar2=None, op0=MULT)
                 nc.vector.tensor_scalar(out=xhat[:, i, :], in0=xhat[:, i, :], scalar1=mut[:, i : i + 1], scalar2=rt[:, i : i + 1], op0=SUB, op1=MULT)
             elif k == "la":
-                lt[i] = e = work.tile([128, R], F32, name="e")
-                nc.vector.scalar_tensor_tensor(out=e[:], in0=dh[i][:], scalar=rt[:, i : i + 1], in1=gB[:], op0=MULT, op1=MULT, accum_out=sums[:, i, 0:1])
+                ee = work.tile([128, 2, R], F32, name="ee", tag="f", bufs=3)
+                lt[i] = e = ee[:, 0, :]
+                ex[i] = ee[:, 1, :]
+                nc.vector.scalar_tensor_tensor(out=e, in0=dh[i][:], scalar=rs[:, i : i + 1], in1=gB[:], op0=MULT, op1=MULT, accum_out=sums[:, i, 0:1])
+                if i == 3:
+                    late.append(0)
             elif k == "lb":
-                ex[i] = z = work.tile([128, R], F32, name="ex")
-                nc.vector.scalar_tensor_tensor(out=z[:], in0=lt[i][:], scalar=1.0, in1=xhat[:, i, :], op0=MULT, op1=MULT, accum_out=sums[:, i, 1:2])
+                nc.vector.scalar_tensor_tensor(out=ex[i], in0=lt[i], scalar=1.0, in1=xhat[:, i, :], op0=MULT, op1=MULT, accum_out=sums[:, i, 1:2])
+            elif k == "lc" and a[1:] == ["S"]:
+                nc.scalar.activation(out=ex[i], in_=xhat[:, i, :], func=mybir.ActivationFunctionType.Identity, scale=sums[:, i, 1:2], bias=sums[:, i, 0:1])
             elif k == "lc":
-                nc.vector.tensor_scalar(out=sums[:, i, :], in0=sums[:, i, :], scalar1=1.0 / R, scalar2=None, op0=MULT)
-                nc.vector.tensor_scalar(out=ex[i][:], in0=xhat[:, i, :], scalar1=sums[:, i, 1:2], scalar2=sums[:, i, 0:1], op0=MULT, op1=ADD)
+                nc.vector.tensor_scalar(out=ex[i], in0=xhat[:, i, :], scalar1=sums[:, i, 1:2], scalar2=sums[:, i, 0:1], op0=MULT, op1=ADD)
             elif k == "ld":
-                nc.vector.tensor_tensor(out=dc[:, i, :], in0=lt[i][:], in1=ex[i][:], op=SUB)
+                nc.vector.scalar_tensor_tensor(out=dc[:, i, :], in0=lt[i], scalar=float(R), in1=ex[i], op0=MULT, op1=SUB)
             else:
                 assert 0, name
 
         dh, stage = {}, {}
+        pend, late = [], []
 
-        def mm(acc, l, ls, r, rs, fl, fr, start, stop):
-            nc.tensor.matmul_mx(out=acc, lhsT=l.bitcast(fl), lhsT_scale=ls, rhs=r.bitcast(fr), rhs_scale=rs, start=start, stop=stop)
-
-        pend = []
+        def mm(acc, l, ls, r, rs_, fl, fr, start, stop):
+            nc.tensor.matmul_mx(out=acc, lhsT=l.bitcast(fl), lhsT_scale=ls, rhs=r.bitcast(fr), rhs_scale=rs_, start=start, stop=stop)
 
         def bank():
-            if len(pend) == NACC:
+            if len(pend) == NACC + len(late[:1]):
                 drain(*pend.pop(0))
-            t = ps.tile([128, 512], F32, name="acc", bufs=NACC)
+            if late:
+                late.append(0)
+            if late and len(late) % (NACC + 1) == 0:
+                t = ps.tile([128, 512], F32, name="dh", bufs=1)
+            else:
+                t = ps.tile([128, 512], F32, name="acc", bufs=NACC)
             return t
 
         def mtask(name):
@@ -304,17 +303,14 @@ def tile_mla_pa_v_kernel(
                 acc = bank()
                 nc.tensor.matmul(acc[:], ones[:], gz[:], start=True, stop=True)
                 pend.append((acc, None, eng[0]))
-                return
-            if k == "dh":
-                j, lo, hi = a
-                if lo == 0:
-                    acc = ps.tile([128, 512], F32, name="dh", bufs=1)
-                    dh[j] = acc
+            elif k == "dh":
+                j = a[0]
+                acc = ps.tile([128, 512], F32, name="dh", bufs=1)
+                dh[j] = acc
                 codes, scales = zc[j]
-                for i in range(lo, hi):
-                    mm(dh[j][:], codes[:, i, :], scales[:, i, :], w2c[:, i, :], w2s[:, i, :], E5, E4, i == 0, i == 7)
-                return
-            if k in "Al":
+                for i in range(8):
+                    mm(acc[:], codes[:, i, :], scales[:, i, :], w2c[:, i, :], w2s[:, i, :], E5, E4, i == 0, i == 7)
+            elif k in "Al":
                 m = a[0]
                 for n in (0, 1) if k == "A" else (2,):
                     acc = bank()
@@ -323,8 +319,10 @@ def tile_mla_pa_v_kernel(
             else:
                 n, j = a
                 acc = bank()
+                cols = slice(512 * n, 512 * n + 512)
                 for g in range(3):
-                    mm(acc[:], fc[:, j, g, :], fs[:, j, g, :], kc[:, g, 512 * n : 512 * n + 512], ks[:, g, 512 * n : 512 * n + 512], E5, E4, g == 0, g == 2)
+                    l, ls = (fc[:, j, g, :], fs[:, j, g, :]) if g < 2 else (dcod[:, j, :], dsc[:, j, :])
+                    mm(acc[:], l, ls, kc[:, g, cols], ks[:, g, cols], E5, E4, g == 0, g == 2)
                 pend.append((acc, ("o", j, n), eng[0]))
 
         def drain(acc, key, eng):
@@ -332,50 +330,54 @@ def tile_mla_pa_v_kernel(
                 put(eng, gB[:], acc[:])
                 return
             k, m, n = key
-            sk, idx = (("A", m // 2), 2 * (m % 2) + n) if k == "A" else (("l", m // 4), m % 4) if k == "l" else (("o", n), m)
+            sk, idx = (("A", m), n) if k == "A" else (("l", m // 2), m % 2) if k == "l" else (("o", m, n // 2), n % 2)
             if sk not in stage:
-                t = big.tile([128, 4, 512], F32, name="big", align_bytes=64)
+                t = outp.tile([128, 2, 512], F32, name="out", align_bytes=64)
                 stage[sk] = [t, 0]
             st = stage[sk]
             put(eng, st[0][:, idx, :], acc[:])
             st[1] += 1
-            fine = sk in FINE
-            if st[1] == 4 or (fine and st[1] == 2):
-                lo = 2 if fine and st[1] == 4 else 0
-                hi = 2 if fine and st[1] == 2 else 4
-                i = sk[1]
+            if k == "o" and n in FINE:
+                nc.sync.dma_start(out=o0v[:, m, 512 * n : 512 * n + 512], in_=st[0][:, idx, :])
+            elif st[1] == 2:
+                flat = st[0][:].rearrange("p a w -> p (a w)")
                 if k == "A":
-                    nc.sync.dma_start(out=o1v[:, 2 * i : 2 * i + 2, 0:1024], in_=st[0][:].rearrange("p (m n) w -> p m (n w)", m=2))
+                    nc.sync.dma_start(out=o1v[:, m, 0:1024], in_=flat)
                 elif k == "l":
-                    nc.sync.dma_start(out=o1v[:, 4 * i + lo : 4 * i + hi, 1024:1536], in_=st[0][:, lo:hi, :])
+                    nc.sync.dma_start(out=o1v[:, m // 2 * 2 : m // 2 * 2 + 2, 1024:1536], in_=st[0][:])
                 else:
-                    nc.sync.dma_start(out=o0v[:, lo:hi, 512 * i : 512 * i + 512], in_=st[0][:, lo:hi, :])
+                    nc.sync.dma_start(out=o0v[:, m, 1024 * (n // 2) : 1024 * (n // 2) + 1024], in_=flat)
 
         ctx.enter_context(tc.manual_schedule())
         last = {}
-        for r, (run, vs, ms) in enumerate(ROWS):
-            for u in run:
-                for key in unit_keys(u):
-                    last[key] = r
+        split = ["k" + v.split()[1] for row in ROWS for v in row[2] if v[0:2] == "d "]
+        for r, (run, engs, vs, ms) in enumerate(ROWS):
+            if run:
+                for key in run_keys(run):
+                    if key not in split:
+                        last[key] = r
+            for v in vs:
+                if v[0:2] == "d ":
+                    last["k" + v.split()[1]] = r
+                if v[0:2] == "xi":
+                    last["x" + v.split()[1]] = r
         loads, issued = list(LOADS), []
-        prev = []
-        for r, (run, vs, ms) in enumerate(ROWS):
+        prev = None
+        for r, (run, engs, vs, ms) in enumerate(ROWS):
             while loads:
-                if loads[0][0] in "wabk":
+                if loads[0][0] in "wakx":
                     if len(issued) >= NRAW and last[issued[-NRAW]] >= r:
                         break
                     issued.append(loads[0])
                 load(loads.pop(0))
-            cur = [transposes(u) for u in run]
+            cur = transposes(run) if run else None
             while pend:
                 drain(*pend.pop(0))
-            for h in prev:
-                quantize(h)
-            for h in cur:
-                empty(h, "S")
-            prev = cur
+            if prev:
+                quantize(prev)
+            prev = (empty(cur[0], engs), len(cur[0]), cur[1], cur[2]) if cur else None
             for m in ms:
                 mtask(m)
             for v in vs:
-                vtask(v, dh)
+                vtask(v)
         assert not prev and not pend and not loads

@@ -7,54 +7,73 @@ F32 = mybir.dt.float32
 BF16 = mybir.dt.bfloat16
 U32 = mybir.dt.uint32
 U8 = mybir.dt.uint8
-E4 = mybir.dt.float8_e4m3fn_x4
-E5 = mybir.dt.float8_e5m2_x4
+E4M3 = mybir.dt.float8_e4m3fn_x4
+E5M2 = mybir.dt.float8_e5m2_x4
 MULT = mybir.AluOpType.mult
 ADD = mybir.AluOpType.add
 SUB = mybir.AluOpType.subtract
 
-T, DIM, R, HN, HV, HR, W = 512, 2048, 512, 2048, 2048, 1024, 1536
-FLOPS = 2 * (T * (HN + HV) * R + 2 * T * W * DIM)
-BYTES = 2 * (T * DIM + DIM * W + R * (HN + HV) + T * (HN + HR + HV) + 256 * 64 + R) + 4 * (T * R + 2 * T) + 4 * (T * DIM + DIM * W)
-NRAW, NTP, NACC, NOUT, NSTG, NKD, NZ = 10, 4, 3, 6, 3, 3, 3
-FINE = ()
-LOADS = ["g0","t","a0","g2","x1","w5","s","w4","g1","w6","w7","w0","g3","x0","w1","w2","w3","x2","a2","a3","c","k9","k6","a1","k7","x3","k10","k8","k11","k14","k5","k0","k2","k3","k13","k1","k12","k15","k4"]
-ROWS = [
-    ("", "VV", ["tab","ra 0","rc 0"], []),
-    ("Z 0 1", "SS", ["xi 1 S","ra 2","rc 2"], []),
-    ("Z 0 0", "SS", ["ra 1"], []),
-    ("Z 2 0", "SS", ["rc 1"], []),
-    ("W 5", "SS", [], []),
-    ("W 6", "SS", [], []),
-    ("W 4", "SS", ["xq 1"], []),
-    ("W 7", "SS", [], []),
-    ("F 0", "SS", ["ra 3"], []),
-    ("Z 1 0", "SS", [], ["gb S"]),
+TOKENS, DIM, RANK, HEADS, HEAD = 512, 2048, 512, 16, 192
+NOPE, ROPE = 2048, 1024
+FEATURES = 4096
+WIDTH = ROPE + RANK
+FLOPS = 2 * (TOKENS * FEATURES * RANK + 2 * TOKENS * WIDTH * DIM)
+BYTES = (
+    2 * (TOKENS * DIM + DIM * WIDTH + RANK * FEATURES + TOKENS * (FEATURES + ROPE) + 256 * 64 + RANK)
+    + 4 * (TOKENS * RANK + 2 * TOKENS)
+    + 4 * (TOKENS * DIM + DIM * WIDTH)
+)
+
+INPUT_BUFS = 10
+OUT_BUFS = 6
+SPLIT_BUFS = 3
+DZ2_BUFS = 3
+TURNED_BUFS = 3
+TURN_BANKS = 4
+PRODUCT_BANKS = 3
+
+LOADS = [
+    "t", "g 0", "w 4", "g 2", "w 5", "w 6", "w 7", "g 1", "w 0", "k 5", "s", "x 0", "g 3", "w 1",
+    "w 2", "w 3", "a 0", "x 1", "k 12", "a 2", "k 2", "c", "a 1", "x 3", "a 3", "k 1", "x 2", "k 0",
+    "k 3", "k 7", "k 10", "k 6", "k 4", "k 15", "k 13", "k 14", "k 11", "k 8", "k 9",
+]
+
+STEPS = [
+    ("W 4", "SS", ["tables", "turn 0", "sum 0", "turn 2", "sum 2"], []),
+    ("W 5", "SS", ["turn 1"], []),
+    ("Z 2 0", "SS", [], []),
+    ("W 6", "SS", [], ["gain S"]),
+    ("W 7", "SS", ["sum 1", "xlay 0 S"], []),
+    ("Z 0 0", "VS", ["turn 3"], []),
+    ("F 0", "SS", ["xquant 0"], []),
+    ("W 0", "SS", [], []),
+    ("W 1", "SS", ["sum 3"], []),
     ("W 2", "SS", [], []),
-    ("W 0", "SS", ["rc 3"], []),
-    ("W 1", "SS", ["xi 0 V"], []),
-    ("W 3", "SS", ["xh 0"], []),
-    ("Z 2 1", "SS", ["xh 1"], []),
-    ("Z 3 1", "SS", ["d 9 V","xh 2","la 0","xi 2 S","xq 0","xq 2","d 7 S"], ["dh 0"]),
-    ("", "VV", [], []),
-    ("Z 1 1", "SS", ["lb 0"], []),
-    ("Z 3 0", "SS", ["lc 0 V","xi 3 V","la 1","d 6 V","ti 0 S","xq 3"], ["dh 1"]),
-    ("K 2 0", "SS", [], []),
-    ("K 2 1", "SS", ["ld 0","xh 3","ti 1 S","la 2","lb 1","tq 0","lc 1 S","tq 1"], ["dh 2"]),
-    ("K 2 2", "SS", ["la 3","d 5 S","lb 2","lb 3","ld 1","lc 2 V"], ["dh 3"]),
-    ("K 0 1", "SS", ["lc 3 V"], ["A 8 S S","A 4 S S","A 6 V S"]),
-    ("K 1 1", "SV", [], ["A 9 V S","A 11 V S"]),
-    ("F 1", "SS", ["ld 2","ld 3"], ["A 1 V S","A 3 S S"]),
-    ("K 0 2", "SV", [], ["A 10 S S","A 13 V V"]),
-    ("D", "SS", [], ["A 12 V S","A 14 S S"]),
-    ("K 0 0", "SS", ["ti 2 V"], ["A 15 S V"]),
-    ("K 3 0", "SS", ["tq 2"], ["A 7 V S"]),
-    ("K 3 1", "SV", [], ["l 9 V","l 8 S","A 5 S V"]),
-    ("K 1 0", "SS", [], ["A 0 S V","l 5 S","l 4 V"]),
-    ("K 3 2", "SV", [], []),
-    ("K 1 2", "SV", [], ["l 12 S"]),
-    ("", "VS", [], ["l 13 S","A 2 S S","o 0 1 V","o 0 2 S","l 0 V","l 1 S","o 1 1 S","l 15 V","o 1 2 S","l 7 V","o 3 0 S","l 14 V","l 6 V","o 2 0 S","o 1 3 S","o 0 3 V","l 11 V","l 3 V","l 2 V","o 2 3 V","o 3 2 S","o 2 2 S","l 10 S","o 1 0 S","o 3 3 S","o 0 0 V","o 2 1 S","o 3 1 V"]),
-    ("", "VS", [], []),
+    ("Z 0 1", "SS", [], []),
+    ("W 3", "SS", ["xlay 1 V"], []),
+    ("Z 2 1", "SS", ["xhat 0", "split 5 V"], []),
+    ("Z 1 0", "SS", ["zlay 1 S", "xquant 1", "xhat 2", "norm1 0"], ["dh 0"]),
+    ("Z 1 1", "SV", ["split 12 V", "zquant 1", "zlay 0 S"], []),
+    ("Z 3 0", "SS", ["zquant 0", "norm1 2", "norm2 0", "norm2 2", "norm3 0", "xlay 2 S", "norm3 2"], ["dh 2"]),
+    ("", "", ["xquant 2", "xlay 3 V"], []),
+    ("K 0 0", "SS", [], ["A 4 S S", "dh 1"]),
+    ("Z 3 1", "SS", ["xquant 3", "xhat 1", "norm1 1", "norm4 0"], ["A 5 S S"]),
+    ("K 0 1", "SS", [], []),
+    ("K 0 2", "SS", ["norm2 1"], ["A 8 S S"]),
+    ("", "", ["norm1 3"], ["dh 3", "A 0 S S"]),
+    ("K 1 0", "SS", ["xhat 3", "norm4 2", "norm2 3"], ["A 6 S V", "A 12 V S"]),
+    ("K 1 1", "VS", ["norm3 1"], ["A 7 V S", "A 13 S S"]),
+    ("K 2 0", "VS", ["norm3 3"], ["A 1 V S", "A 9 S S"]),
+    ("F 1", "SS", ["norm4 1"], ["A 2 V V", "A 10 S V"]),
+    ("K 3 0", "SS", ["norm4 3"], []),
+    ("K 2 1", "VS", ["zlay 2 V"], ["A 3 S S", "A 11 S S"]),
+    ("D", "VS", ["zquant 2"], ["A 14 S V", "A 15 V S"]),
+    ("K 2 2", "SS", [], []),
+    ("K 1 2", "SV", [], ["l 0 S", "l 1 S", "l 2 V"]),
+    ("K 3 1", "SV", [], ["l 3 S", "l 4 S", "l 5 V"]),
+    ("K 3 2", "SS", [], ["l 6 S", "l 7 V"]),
+    ("", "", [], ["o 0 3 S", "o 1 3 S", "l 8 V", "l 9 V", "o 1 1 S", "l 10 V", "o 0 1 S", "l 11 V", "o 2 3 S", "l 12 V", "l 13 S", "o 3 3 V", "o 0 2 V", "o 1 2 S", "o 2 1 V", "l 14 V", "l 15 S", "o 1 0 V", "o 0 0 S", "o 2 0 V", "o 3 0 S", "o 3 1 S", "o 3 2 S", "o 2 2 S"]),
+    ("", "", [], []),
 ]
 
 
@@ -62,322 +81,323 @@ def tile_mla_pa_v_kernel(
     tc, x, wkv_a_w, wkv_a_b, kvn_g, kvn_b, wk_w, wk_b, wv_w, wv_b, cos, sin, c_lat, mu, rstd, grad_0, grad_1, out_0, out_1
 ):
     nc = tc.nc
-    xv = x.flatten_outer_dims().rearrange("(p j) w -> p j w", j=4)
-    g0v = grad_0.rearrange("b s h d -> (b s) (h d)").rearrange("(p j) w -> p j w", j=4)
-    g1v = grad_1.rearrange("b s h d -> (b s) (h d)").rearrange("(p j) w -> p j w", j=4)
-    cv = c_lat.flatten_outer_dims().rearrange("(p j) w -> p j w", j=4)
-    muv = mu.flatten_outer_dims().rearrange("(p j) o -> p (j o)", j=4)
-    rv = rstd.flatten_outer_dims().rearrange("(p j) o -> p (j o)", j=4)
-    cosv = cos.rearrange("(q j) w -> q j w", j=4)
-    sinv = sin.rearrange("(q j) w -> q j w", j=4)
-    o0v = out_0.flatten_outer_dims().rearrange("(p j) w -> p j w", j=4)
-    o1v = out_1.rearrange("(m p) w -> p m w", p=128)
+    x_rows = x.flatten_outer_dims().rearrange("(p j) w -> p j w", j=4)
+    grad_0_rows = grad_0.rearrange("b s h d -> (b s) (h d)").rearrange("(p j) w -> p j w", j=4)
+    grad_1_rows = grad_1.rearrange("b s h d -> (b s) (h d)").rearrange("(p j) w -> p j w", j=4)
+    c_lat_rows = c_lat.flatten_outer_dims().rearrange("(p j) w -> p j w", j=4)
+    mu_rows = mu.flatten_outer_dims().rearrange("(p j) o -> p (j o)", j=4)
+    rstd_rows = rstd.flatten_outer_dims().rearrange("(p j) o -> p (j o)", j=4)
+    out_0_rows = out_0.flatten_outer_dims().rearrange("(p j) w -> p j w", j=4)
+    out_1_rows = out_1.rearrange("(m p) w -> p m w", p=128)
+    cos_rows = cos.rearrange("(q j) w -> q j w", j=4)
+    sin_rows = sin.rearrange("(q j) w -> q j w", j=4)
 
     with ExitStack() as ctx:
         keep = ctx.enter_context(tc.tile_pool(name="keep", bufs=1))
-        rawp = ctx.enter_context(tc.tile_pool(name="rawp", bufs=NRAW))
-        outp = ctx.enter_context(tc.tile_pool(name="outp", bufs=NOUT))
-        stgp = ctx.enter_context(tc.tile_pool(name="stgp", bufs=NSTG))
+        inputs = ctx.enter_context(tc.tile_pool(name="inputs", bufs=INPUT_BUFS))
+        outputs = ctx.enter_context(tc.tile_pool(name="outputs", bufs=OUT_BUFS))
+        turned = ctx.enter_context(tc.tile_pool(name="turned", bufs=TURNED_BUFS))
         work = ctx.enter_context(tc.tile_pool(name="work", bufs=2))
-        ps = ctx.enter_context(tc.psum_pool(name="ps", bufs=3))
+        psum = ctx.enter_context(tc.psum_pool(name="psum", bufs=1))
 
-        def kt(name, shape, dt):
-            return keep.tile(shape, dt, name=name, align_bytes=64)
+        def kept(name, shape, dtype):
+            return keep.tile(shape, dtype, name=name, align_bytes=64)
 
-        ident = kt("ident", [128, 128], F32)
-        make_identity(nc, ident[:])
-        ones = kt("ones", [128, 128], BF16)
+        identity = kept("identity", [128, 128], F32)
+        make_identity(nc, identity[:])
+        ones = kept("ones", [128, 128], BF16)
         nc.gpsimd.memset(ones[:], 1.0)
-        gz = kt("gz", [128, R], BF16)
-        nc.gpsimd.memset(gz[:], 0.0)
-        cosb = kt("cosb", [128, 4, 32], BF16)
-        sinb = kt("sinb", [128, 4, 32], BF16)
-        mut = kt("mut", [128, 4], F32)
-        rt = kt("rt", [128, 4], F32)
-        rs = kt("rs", [128, 4], F32)
-        w2c = kt("w2c", [128, 8, R], U32)
-        w2s = kt("w2s", [128, 8, R], U8)
-        xc = kt("xc", [128, DIM], U32)
-        xs = kt("xs", [128, DIM], U8)
-        kc = kt("kc", [128, 3, DIM], U32)
-        ks = kt("ks", [128, 3, DIM], U8)
-        tcod = kt("tcod", [128, W], U32)
-        tsc = kt("tsc", [128, W], U8)
-        fc = kt("fc", [128, 4, 2, 128], U32)
-        fs = kt("fs", [128, 4, 2, 128], U8)
-        dcod = kt("dcod", [128, 4, 128], U32)
-        dsc = kt("dsc", [128, 4, 128], U8)
-        g0 = kt("g0", [128, 4, 3072], BF16)
-        xhat = kt("xhat", [128, 4, R], F32)
-        dc = kt("dc", [128, 4, R], BF16)
-        gB = kt("gB", [128, R], F32)
-        c2 = kt("c2", [128, 4, 32, 2], BF16)
-        s2 = kt("s2", [128, 4, 32, 2], BF16)
-        sums = kt("sums", [128, 4, 2], F32)
-        c2f = c2[:].rearrange("p j w e -> p j (w e)")
-        s2f = s2[:].rearrange("p j w e -> p j (w e)")
+        gain_row = kept("gain_row", [128, RANK], BF16)
+        nc.gpsimd.memset(gain_row[:], 0.0)
+        cos_in = kept("cos_in", [128, 4, 32], BF16)
+        sin_in = kept("sin_in", [128, 4, 32], BF16)
+        mu_col = kept("mu_col", [128, 4], F32)
+        rstd_col = kept("rstd_col", [128, 4], F32)
+        rstd_mean_col = kept("rstd_mean_col", [128, 4], F32)
+        w2_codes = kept("w2_codes", [128, 8, RANK], U32)
+        w2_scales = kept("w2_scales", [128, 8, RANK], U8)
+        x_codes = kept("x_codes", [128, DIM], U32)
+        x_scales = kept("x_scales", [128, DIM], U8)
+        wkv_codes = kept("wkv_codes", [128, 3, DIM], U32)
+        wkv_scales = kept("wkv_scales", [128, 3, DIM], U8)
+        dz1_token_codes = kept("dz1_token_codes", [128, WIDTH], U32)
+        dz1_token_scales = kept("dz1_token_scales", [128, WIDTH], U8)
+        rope_codes = kept("rope_codes", [128, 4, 2, 128], U32)
+        rope_scales = kept("rope_scales", [128, 4, 2, 128], U8)
+        latent_codes = kept("latent_codes", [128, 4, 128], U32)
+        latent_scales = kept("latent_scales", [128, 4, 128], U8)
+        g0 = kept("g0", [128, 4, HEADS * HEAD], BF16)
+        xhat = kept("xhat", [128, 4, RANK], F32)
+        dc = kept("dc", [128, 4, RANK], BF16)
+        gain = kept("gain", [128, RANK], F32)
+        cos_pairs = kept("cos_pairs", [128, 4, 32, 2], BF16)
+        sin_pairs = kept("sin_pairs", [128, 4, 32, 2], BF16)
+        means = kept("means", [128, 4, 2], F32)
 
-        def put(eng, out, in_):
-            if eng == "V":
+        def copy(engine, out, in_):
+            if engine == "V":
                 nc.vector.tensor_copy(out=out, in_=in_)
             else:
                 nc.scalar.copy(out=out, in_=in_)
 
-        raw = {}
+        loaded = {}
 
         def load(name):
-            k = name[0]
-            i = int(name[1:] or 0)
-            if k in "wakx":
-                t = rawp.tile([128, 2048], BF16, name="raw", align_bytes=64)
-                raw[name] = t
+            k, *rest = name.split()
+            i = int(rest[0]) if rest else 0
+            if k == "x":
+                t = outputs.tile([128, 4, 512], BF16, name="out", align_bytes=64)
+                loaded[name] = t
+                nc.sync.dma_start(out=t[:], in_=x_rows[:, :, 512 * i : 512 * i + 512])
+            elif k in "wak":
+                t = inputs.tile([128, 2048], BF16, name="input", align_bytes=64)
+                loaded[name] = t
                 if k == "k":
-                    nc.sync.dma_start(out=t[:, 0:W], in_=wkv_a_w[128 * i : 128 * i + 128, :])
-                elif k == "x":
-                    nc.sync.dma_start(out=t[:].rearrange("p (j c) -> p j c", j=4), in_=xv[:, :, 512 * i : 512 * i + 512])
+                    nc.sync.dma_start(out=t[:, 0:WIDTH], in_=wkv_a_w[128 * i : 128 * i + 128, :])
                 elif k == "a":
-                    nc.sync.dma_start(out=t[:], in_=g1v[:, i, :])
+                    nc.sync.dma_start(out=t[:], in_=grad_1_rows[:, i, :])
                 else:
                     w = wk_w if i < 4 else wv_w
                     nc.sync.dma_start(out=t[:], in_=w[128 * (i % 4) : 128 * (i % 4) + 128, :])
             elif k == "g":
-                nc.sync.dma_start(out=g0[:, i, :], in_=g0v[:, i, :])
+                nc.sync.dma_start(out=g0[:, i, :], in_=grad_0_rows[:, i, :])
             elif k == "c":
-                nc.sync.dma_start(out=xhat[:], in_=cv)
+                nc.sync.dma_start(out=xhat[:], in_=c_lat_rows)
             elif k == "t":
-                for h in range(2):
-                    nc.sync.dma_start(out=cosb[64 * h : 64 * h + 64], in_=cosv)
-                    nc.sync.dma_start(out=sinb[64 * h : 64 * h + 64], in_=sinv)
+                for half in (slice(0, 64), slice(64, 128)):
+                    nc.sync.dma_start(out=cos_in[half], in_=cos_rows)
+                    nc.sync.dma_start(out=sin_in[half], in_=sin_rows)
             elif k == "s":
-                nc.sync.dma_start(out=mut[:], in_=muv)
-                nc.sync.dma_start(out=rt[:], in_=rv)
-                nc.sync.dma_start(out=gz[0:1, :], in_=kvn_g.rearrange("(o w) -> o w", o=1))
+                nc.sync.dma_start(out=mu_col[:], in_=mu_rows)
+                nc.sync.dma_start(out=rstd_col[:], in_=rstd_rows)
+                nc.sync.dma_start(out=gain_row[0:1, :], in_=kvn_g.rearrange("(o w) -> o w", o=1))
 
-        zc, kd = {}, {}
+        def buffered(name):
+            return name[0] in "wak"
 
-        def run_keys(name):
-            k, *a = name.split()
-            a = [int(z) for z in a]
-            if k in "WK":
-                return [("w%d" if k == "W" else "k%d") % (4 * (a[0] // 4 if k == "W" else a[0]) + i) for i in range(4)]
-            return ["a%d" % a[0]] if k == "Z" and a[1] else []
+        dz2, split = {}, {}
 
-        def run_of(name):
-            k, *a = name.split()
+        def run_inputs(run):
+            k, *a = run.split()
+            if k == "W":
+                first = 4 * (int(a[0]) // 4)
+                return ["w %d" % (first + i) for i in range(4)]
+            if k == "K":
+                return ["k %d" % (4 * int(a[0]) + i) for i in range(4)]
+            return ["a " + a[0]] if k == "Z" and a[1] == "1" else []
+
+        def words(rows, g):
+            return rows.bitcast(F32)[:, 256 * g : 256 * g + 256].rearrange("p (w u) -> p u w", u=2)
+
+        def run_blocks(run):
+            k, *a = run.split()
             a = [int(z) for z in a]
             if k == "W":
-                g = a[0]
-                return [raw[q][:].bitcast(F32)[:, 256 * (g % 4) : 256 * (g % 4) + 256] for q in run_keys(name)], (lambda: (w2c[:, g, :], w2s[:, g, :])), E4
+                return [words(loaded[name][:], a[0] % 4) for name in run_inputs(run)]
             if k == "K":
-                n, g = a
-                cols = slice(512 * n, 512 * n + 512)
-                return [kd[q][:, g, :, :] if q in kd else raw[q][:].bitcast(F32)[:, 256 * g : 256 * g + 256] for q in run_keys(name)], (lambda: (kc[:, g, cols], ks[:, g, cols])), E4
+                return [split[name][:, a[1], :, :] if name in split else words(loaded[name][:], a[1]) for name in run_inputs(run)]
             if k == "Z":
-                j, half = a
-
-                def dst():
-                    if j not in zc:
-                        codes = work.tile([128, 8, 128], U32, name="zcod", bufs=NZ, align_bytes=64)
-                        scales = work.tile([128, 8, 128], U8, name="zsc", bufs=NZ, align_bytes=64)
-                        zc[j] = (codes, scales)
-                    return [t[:, 4 * half : 4 * half + 4, :].rearrange("p a n -> p (a n)") for t in zc[j]]
-
-                wd = (raw["a%d" % j][:] if half else g0[:, j, 0:2048]).bitcast(F32)
-                return [wd[:, 256 * i : 256 * i + 256] for i in range(4)], dst, E5
+                rows = loaded["a %d" % a[0]][:] if a[1] else g0[:, a[0], 0:NOPE]
+                return [words(rows, g) for g in range(4)]
             if k == "F":
-                wd = [g0[:, 2 * a[0] + i, 2048:3072].bitcast(F32) for i in range(2)]
-                return [wd[i // 2][:, 256 * (i % 2) : 256 * (i % 2) + 256] for i in range(4)], (lambda: [t[:, 2 * a[0] : 2 * a[0] + 2, :, :].rearrange("p j g n -> p (j g n)") for t in (fc, fs)]), E5
-            if k == "D":
-                jj = [2 * a[0], 2 * a[0] + 1] if a else [0, 1, 2, 3]
-                return [dc[:, j, :].bitcast(F32) for j in jj], (lambda: [t[:, jj[0] : jj[-1] + 1, :].rearrange("p j n -> p (j n)") for t in (dcod, dsc)]), E5
+                return [words(g0[:, 2 * a[0] + i, NOPE : NOPE + ROPE], g) for i in range(2) for g in range(2)]
+            return [words(dc[:, j, :], 0) for j in range(4)]
 
-        def transposes(name):
-            src, dst, fmt = run_of(name)
+        def run_operand(run):
+            k, *a = run.split()
+            a = [int(z) for z in a]
+            if k == "W":
+                return w2_codes[:, a[0], :], w2_scales[:, a[0], :], E4M3
+            if k == "K":
+                cols = slice(512 * a[0], 512 * a[0] + 512)
+                return wkv_codes[:, a[1], cols], wkv_scales[:, a[1], cols], E4M3
+            if k == "Z":
+                j, h = a
+                if j not in dz2:
+                    codes = work.tile([128, 8, 128], U32, name="dz2_codes", bufs=DZ2_BUFS, align_bytes=64)
+                    scales = work.tile([128, 8, 128], U8, name="dz2_scales", bufs=DZ2_BUFS, align_bytes=64)
+                    dz2[j] = (codes, scales)
+                codes, scales = [t[:, 4 * h : 4 * h + 4, :].rearrange("p g n -> p (g n)") for t in dz2[j]]
+                return codes, scales, E5M2
+            if k == "F":
+                tiles = slice(2 * a[0], 2 * a[0] + 2)
+                codes, scales = [t[:, tiles, :, :].rearrange("p j g n -> p (j g n)") for t in (rope_codes, rope_scales)]
+                return codes, scales, E5M2
+            codes, scales = [t[:].rearrange("p j n -> p (j n)") for t in (latent_codes, latent_scales)]
+            return codes, scales, E5M2
+
+        def transpose_run(run):
+            blocks = run_blocks(run)
             banks = []
-            for b in range(len(src) // 2):
-                bk = ps.tile([128, 2, 2, 128], F32, name="tp", bufs=NTP)
-                banks.append(bk)
+            for b in range(2):
+                bank = psum.tile([128, 2, 2, 128], F32, name="turn", bufs=TURN_BANKS)
+                banks.append(bank)
                 for a in range(2):
                     for u in range(2):
-                        s = src[2 * b + a]
-                        nc.tensor.transpose(bk[:, a, u, :], s[:, u, :] if len(s.shape) == 3 else s[:, u::2], ident[:])
-            return banks, dst, fmt
+                        nc.tensor.transpose(bank[:, a, u, :], blocks[2 * b + a][:, u, :], identity[:])
+            return banks
 
-        def empty(banks, engs):
-            stg = stgp.tile([128, 4, 128, 4], BF16, name="stg", align_bytes=64)
-            for b, bk in enumerate(banks):
-                put(engs[b], stg[:, 2 * b : 2 * b + 2, :, :].bitcast(F32), bk[:].rearrange("p a u n -> p a n u"))
-            return stg
+        def copy_run(banks, engines):
+            rows = turned.tile([128, 4, 128, 4], BF16, name="rows", align_bytes=64)
+            for b in range(2):
+                copy(engines[b], rows[:, 2 * b : 2 * b + 2, :, :].bitcast(F32), banks[b][:].rearrange("p a u n -> p a n u"))
+            return rows
 
-        def quantize(h):
-            stg, nb, dst, fmt = h
-            codes, scales = dst()
-            nc.vector.quantize_mx(out=codes.bitcast(fmt), scales=scales, in_=stg[:, 0 : 2 * nb, :, :].rearrange("p a n t -> p (a n t)"))
+        def quantize_run(run, rows):
+            codes, scales, fmt = run_operand(run)
+            nc.vector.quantize_mx(out=codes.bitcast(fmt), scales=scales, in_=rows[:].rearrange("p a n t -> p (a n t)"))
 
-        ils, lt, ex, rot = {}, {}, {}, {}
+        dh, beside, halves, norm = {}, {}, {}, {}
 
-        def vtask(name):
+        def task(name):
             k, *a = name.split()
             i = int(a[0]) if a else 0
-            if k == "tab":
+            if k == "tables":
                 for e in range(2):
-                    nc.vector.tensor_copy(out=c2[:, :, :, e], in_=cosb[:])
-                nc.vector.tensor_scalar(out=s2[:, :, :, 0], in0=sinb[:], scalar1=-1.0, scalar2=None, op0=MULT)
-                nc.vector.tensor_copy(out=s2[:, :, :, 1], in_=sinb[:])
-            elif k == "ra":
-                seg = g0[:, i, :].rearrange("p (h w) -> p h w", w=192)[:, :, 128:192]
-                m1 = work.tile([128, 16, 64], F32, name="m1", tag="f", bufs=3)
-                nc.vector.tensor_tensor(out=m1[:], in0=seg, in1=c2f[:, i, :].unsqueeze(1).to_broadcast([128, 16, 64]), op=MULT)
-                m2 = work.tile([128, 16, 64], F32, name="m2", tag="f", bufs=3)
-                nc.vector.tensor_tensor(out=m2[:], in0=seg, in1=s2f[:, i, :].unsqueeze(1).to_broadcast([128, 16, 64]), op=MULT)
-                rot[i] = (m1, m2)
-            elif k == "rc":
-                m1, m2 = rot[i]
-                nc.vector.tensor_tensor(
-                    out=g0[:, i, :].rearrange("p (h w) -> p h w", w=192)[:, :, 128:192].rearrange("p h (w e) -> p h w e", e=2),
-                    in0=m1[:].rearrange("p h (w e) -> p h w e", e=2),
-                    in1=m2[:].rearrange("p h (w e) -> p h w e", e=2)[:, :, :, ::-1],
-                    op=ADD,
-                )
-            elif k in ("xi", "ti"):
-                il = work.tile([128, 512, 4], BF16, name="il", align_bytes=64)
-                if k == "xi":
-                    src = raw["x%d" % i][:].rearrange("p (j c) -> p j c", j=4)
-                elif i < 2:
-                    src = g0[:, :, 2048 + 512 * i : 2560 + 512 * i]
+                    nc.vector.tensor_copy(out=cos_pairs[:, :, :, e], in_=cos_in[:])
+                nc.vector.tensor_scalar(out=sin_pairs[:, :, :, 0], in0=sin_in[:], scalar1=-1.0, scalar2=None, op0=MULT)
+                nc.vector.tensor_copy(out=sin_pairs[:, :, :, 1], in_=sin_in[:])
+            elif k == "turn":
+                pairs = g0[:, i, :].rearrange("p (h w) -> p h w", w=HEAD)[:, :, 128:HEAD]
+                halves[i] = []
+                for table in (cos_pairs, sin_pairs):
+                    half = work.tile([128, HEADS, 64], F32, name="half", tag="f32", bufs=3)
+                    halves[i].append(half)
+                    row = table[:, i, :, :].rearrange("p w e -> p (w e)")
+                    nc.vector.tensor_tensor(out=half[:], in0=pairs, in1=row.unsqueeze(1).to_broadcast([128, HEADS, 64]), op=MULT)
+            elif k == "sum":
+                by_cos, by_sin = [half[:].rearrange("p h (w e) -> p h w e", e=2) for half in halves[i]]
+                pairs = g0[:, i, :].rearrange("p (h w) -> p h w", w=HEAD)[:, :, 128:HEAD]
+                nc.vector.tensor_tensor(out=pairs.rearrange("p h (w e) -> p h w e", e=2), in0=by_cos, in1=by_sin[:, :, :, ::-1], op=ADD)
+            elif k in ("xlay", "zlay"):
+                if k == "xlay":
+                    cols = loaded["x %d" % i][:]
                 else:
-                    src = dc[:]
-                put(a[1], il[:], src.rearrange("p j c -> p c j"))
-                ils[(k[0], i)] = il
-            elif k in ("xq", "tq"):
-                codes, scales, fmt = (xc, xs, E4) if k == "xq" else (tcod, tsc, E5)
-                nc.vector.quantize_mx(out=codes[:, 512 * i : 512 * i + 512].bitcast(fmt), scales=scales[:, 512 * i : 512 * i + 512], in_=ils[(k[0], i)][:].rearrange("p c j -> p (c j)"))
-            elif k == "d":
-                t = rawp.tile([128, 3, 2, 128], F32, name="kd", bufs=NKD, align_bytes=64)
-                put(a[1], t[:], raw["k%d" % i][:].bitcast(F32)[:, 0:768].rearrange("p (g w u) -> p g u w", g=3, u=2))
-                kd["k%d" % i] = t
-            elif k == "xh":
+                    cols = g0[:, :, NOPE + 512 * i : NOPE + 512 * i + 512] if i < 2 else dc[:]
+                tokens = work.tile([128, 512, 4], BF16, name="tokens", align_bytes=64)
+                beside[(k[0], i)] = tokens
+                copy(a[1], tokens[:].rearrange("p (c i) j -> p c j i", i=4), cols.rearrange("p j (c i) -> p c j i", i=4))
+            elif k in ("xquant", "zquant"):
+                codes, scales, fmt = (x_codes, x_scales, E4M3) if k == "xquant" else (dz1_token_codes, dz1_token_scales, E5M2)
+                cols = slice(512 * i, 512 * i + 512)
+                nc.vector.quantize_mx(out=codes[:, cols].bitcast(fmt), scales=scales[:, cols], in_=beside[(k[0], i)][:].rearrange("p c j -> p (c j)"))
+            elif k == "split":
+                t = inputs.tile([128, 3, 2, 128], F32, name="split", bufs=SPLIT_BUFS, align_bytes=64)
+                split["k %d" % i] = t
+                copy(a[1], t[:], loaded["k %d" % i][:].bitcast(F32)[:, 0 : WIDTH // 2].rearrange("p (g w u) -> p g u w", g=3, u=2))
+            elif k == "xhat":
                 if i == 0:
-                    nc.vector.tensor_scalar(out=rs[:], in0=rt[:], scalar1=1.0 / R, scalar2=None, op0=MULT)
-                nc.vector.tensor_scalar(out=xhat[:, i, :], in0=xhat[:, i, :], scalar1=mut[:, i : i + 1], scalar2=rt[:, i : i + 1], op0=SUB, op1=MULT)
-            elif k == "la":
-                ee = work.tile([128, 2, R], F32, name="ee", tag="f", bufs=3)
-                lt[i] = e = ee[:, 0, :]
-                ex[i] = ee[:, 1, :]
-                nc.vector.scalar_tensor_tensor(out=e, in0=dh[i][:], scalar=rs[:, i : i + 1], in1=gB[:], op0=MULT, op1=MULT, accum_out=sums[:, i, 0:1])
-                if i == 3:
-                    late.append(0)
-            elif k == "lb":
-                nc.vector.scalar_tensor_tensor(out=ex[i], in0=lt[i], scalar=1.0, in1=xhat[:, i, :], op0=MULT, op1=MULT, accum_out=sums[:, i, 1:2])
-            elif k == "lc" and a[1:] == ["S"]:
-                nc.scalar.activation(out=ex[i], in_=xhat[:, i, :], func=mybir.ActivationFunctionType.Identity, scale=sums[:, i, 1:2], bias=sums[:, i, 0:1])
-            elif k == "lc":
-                nc.vector.tensor_scalar(out=ex[i], in0=xhat[:, i, :], scalar1=sums[:, i, 1:2], scalar2=sums[:, i, 0:1], op0=MULT, op1=ADD)
-            elif k == "ld":
-                nc.vector.scalar_tensor_tensor(out=dc[:, i, :], in0=lt[i], scalar=float(R), in1=ex[i], op0=MULT, op1=SUB)
+                    nc.vector.tensor_scalar(out=rstd_mean_col[:], in0=rstd_col[:], scalar1=1.0 / RANK, scalar2=None, op0=MULT)
+                nc.vector.tensor_scalar(out=xhat[:, i, :], in0=xhat[:, i, :], scalar1=mu_col[:, i : i + 1], scalar2=rstd_col[:, i : i + 1], op0=SUB, op1=MULT)
+            elif k == "norm1":
+                t = work.tile([128, 2, RANK], F32, name="norm", tag="f32", bufs=3)
+                norm[i] = (t[:, 0, :], t[:, 1, :])
+                nc.vector.scalar_tensor_tensor(out=norm[i][0], in0=dh[i][:], scalar=rstd_mean_col[:, i : i + 1], in1=gain[:], op0=MULT, op1=MULT, accum_out=means[:, i, 0:1])
+                if len(norm) == 4:
+                    dh_done.append(True)
+            elif k == "norm2":
+                nc.vector.scalar_tensor_tensor(out=norm[i][1], in0=norm[i][0], scalar=1.0, in1=xhat[:, i, :], op0=MULT, op1=MULT, accum_out=means[:, i, 1:2])
+            elif k == "norm3":
+                nc.vector.tensor_scalar(out=norm[i][1], in0=xhat[:, i, :], scalar1=means[:, i, 1:2], scalar2=means[:, i, 0:1], op0=MULT, op1=ADD)
+            elif k == "norm4":
+                nc.vector.scalar_tensor_tensor(out=dc[:, i, :], in0=norm[i][0], scalar=float(RANK), in1=norm[i][1], op0=MULT, op1=SUB)
+
+        full, dh_done, staged = [], [], {}
+        late_banks = [0]
+
+        def matmul_mx(out, left, right, start, stop):
+            (l, l_scales, l_fmt), (r, r_scales, r_fmt) = left, right
+            nc.tensor.matmul_mx(out=out, lhsT=l.bitcast(l_fmt), lhsT_scale=l_scales, rhs=r.bitcast(r_fmt), rhs_scale=r_scales, start=start, stop=stop)
+
+        def product_bank():
+            if len(full) == PRODUCT_BANKS + len(dh_done):
+                empty(*full.pop(0))
+            if dh_done:
+                late_banks[0] += 1
+            if late_banks[0] % (PRODUCT_BANKS + 1) == PRODUCT_BANKS:
+                bank = psum.tile([128, 512], F32, name="dh")
             else:
-                assert 0, name
+                bank = psum.tile([128, 512], F32, name="product", bufs=PRODUCT_BANKS)
+            return bank
 
-        dh, stage = {}, {}
-        pend, late = [], []
-
-        def mm(acc, l, ls, r, rs_, fl, fr, start, stop):
-            nc.tensor.matmul_mx(out=acc, lhsT=l.bitcast(fl), lhsT_scale=ls, rhs=r.bitcast(fr), rhs_scale=rs_, start=start, stop=stop)
-
-        def bank():
-            if len(pend) == NACC + len(late[:1]):
-                drain(*pend.pop(0))
-            if late:
-                late.append(0)
-            if late and len(late) % (NACC + 1) == 0:
-                t = ps.tile([128, 512], F32, name="dh", bufs=1)
-            else:
-                t = ps.tile([128, 512], F32, name="acc", bufs=NACC)
-            return t
-
-        def mtask(name):
+        def product(name):
             k, *a = name.split()
-            eng = [z for z in a if z in "VS"]
+            engines = [z for z in a if z in "VS"]
             a = [int(z) for z in a if z not in "VS"]
-            if k == "gb":
-                acc = bank()
-                nc.tensor.matmul(acc[:], ones[:], gz[:], start=True, stop=True)
-                pend.append((acc, None, eng[0]))
+            if k == "gain":
+                bank = product_bank()
+                nc.tensor.matmul(bank[:], ones[:], gain_row[:], start=True, stop=True)
+                full.append((bank, None, engines[0]))
             elif k == "dh":
-                j = a[0]
-                acc = ps.tile([128, 512], F32, name="dh", bufs=1)
-                dh[j] = acc
-                codes, scales = zc[j]
-                for i in range(8):
-                    mm(acc[:], codes[:, i, :], scales[:, i, :], w2c[:, i, :], w2s[:, i, :], E5, E4, i == 0, i == 7)
+                bank = psum.tile([128, 512], F32, name="dh")
+                dh[a[0]] = bank
+                codes, scales = dz2[a[0]]
+                for g in range(8):
+                    matmul_mx(bank[:], (codes[:, g, :], scales[:, g, :], E5M2), (w2_codes[:, g, :], w2_scales[:, g, :], E4M3), g == 0, g == 7)
             elif k in "Al":
-                m = a[0]
+                rows = slice(128 * a[0], 128 * a[0] + 128)
                 for n in (0, 1) if k == "A" else (2,):
-                    acc = bank()
-                    mm(acc[:], xc[:, 128 * m : 128 * m + 128], xs[:, 128 * m : 128 * m + 128], tcod[:, 512 * n : 512 * n + 512], tsc[:, 512 * n : 512 * n + 512], E4, E5, True, True)
-                    pend.append((acc, (k, m, n), eng[n % 2]))
-            else:
+                    bank = product_bank()
+                    cols = slice(512 * n, 512 * n + 512)
+                    matmul_mx(bank[:], (x_codes[:, rows], x_scales[:, rows], E4M3), (dz1_token_codes[:, cols], dz1_token_scales[:, cols], E5M2), True, True)
+                    full.append((bank, (k, a[0], n), engines[n % 2]))
+            elif k == "o":
                 n, j = a
-                acc = bank()
+                bank = product_bank()
                 cols = slice(512 * n, 512 * n + 512)
                 for g in range(3):
-                    l, ls = (fc[:, j, g, :], fs[:, j, g, :]) if g < 2 else (dcod[:, j, :], dsc[:, j, :])
-                    mm(acc[:], l, ls, kc[:, g, cols], ks[:, g, cols], E5, E4, g == 0, g == 2)
-                pend.append((acc, ("o", j, n), eng[0]))
+                    left = (rope_codes[:, j, g, :], rope_scales[:, j, g, :], E5M2) if g < 2 else (latent_codes[:, j, :], latent_scales[:, j, :], E5M2)
+                    matmul_mx(bank[:], left, (wkv_codes[:, g, cols], wkv_scales[:, g, cols], E4M3), g == 0, g == 2)
+                full.append((bank, (k, j, n), engines[0]))
 
-        def drain(acc, key, eng):
-            if key is None:
-                put(eng, gB[:], acc[:])
+        def empty(bank, place, engine):
+            if place is None:
+                copy(engine, gain[:], bank[:])
                 return
-            k, m, n = key
-            sk, idx = (("A", m), n) if k == "A" else (("l", m // 2), m % 2) if k == "l" else (("o", m, n // 2), n % 2)
-            if sk not in stage:
-                t = outp.tile([128, 2, 512], F32, name="out", align_bytes=64)
-                stage[sk] = [t, 0]
-            st = stage[sk]
-            put(eng, st[0][:, idx, :], acc[:])
-            st[1] += 1
-            if k == "o" and n in FINE:
-                nc.sync.dma_start(out=o0v[:, m, 512 * n : 512 * n + 512], in_=st[0][:, idx, :])
-            elif st[1] == 2:
-                flat = st[0][:].rearrange("p a w -> p (a w)")
+            k, i, n = place
+            pair, side = {"A": ((k, i), n), "l": ((k, i // 2), i % 2), "o": ((k, i, n // 2), n % 2)}[k]
+            if pair not in staged:
+                t = outputs.tile([128, 2, 512], F32, name="out", align_bytes=64)
+                staged[pair] = [t]
+            t = staged[pair][0]
+            copy(engine, t[:, side, :], bank[:])
+            staged[pair].append(side)
+            if len(staged[pair]) == 3:
                 if k == "A":
-                    nc.sync.dma_start(out=o1v[:, m, 0:1024], in_=flat)
+                    nc.sync.dma_start(out=out_1_rows[:, i, 0:ROPE], in_=t[:].rearrange("p a w -> p (a w)"))
                 elif k == "l":
-                    nc.sync.dma_start(out=o1v[:, m // 2 * 2 : m // 2 * 2 + 2, 1024:1536], in_=st[0][:])
+                    nc.sync.dma_start(out=out_1_rows[:, i // 2 * 2 : i // 2 * 2 + 2, ROPE:WIDTH], in_=t[:])
                 else:
-                    nc.sync.dma_start(out=o0v[:, m, 1024 * (n // 2) : 1024 * (n // 2) + 1024], in_=flat)
+                    nc.sync.dma_start(out=out_0_rows[:, i, 1024 * (n // 2) : 1024 * (n // 2) + 1024], in_=t[:].rearrange("p a w -> p (a w)"))
 
         ctx.enter_context(tc.manual_schedule())
-        last = {}
-        split = ["k" + v.split()[1] for row in ROWS for v in row[2] if v[0:2] == "d "]
-        for r, (run, engs, vs, ms) in enumerate(ROWS):
-            if run:
-                for key in run_keys(run):
-                    if key not in split:
-                        last[key] = r
-            for v in vs:
-                if v[0:2] == "d ":
-                    last["k" + v.split()[1]] = r
-                if v[0:2] == "xi":
-                    last["x" + v.split()[1]] = r
-        loads, issued = list(LOADS), []
-        prev = None
-        for r, (run, engs, vs, ms) in enumerate(ROWS):
-            while loads:
-                if loads[0][0] in "wakx":
-                    if len(issued) >= NRAW and last[issued[-NRAW]] >= r:
+
+        split_names = ["k " + name.split()[1] for step in STEPS for name in step[2] if name.startswith("split")]
+        last_use = {}
+        for s, (run, engines, tasks, products) in enumerate(STEPS):
+            for name in run_inputs(run) if run else []:
+                if name not in split_names:
+                    last_use[name] = s
+            for name in tasks:
+                if name.startswith("split"):
+                    last_use["k " + name.split()[1]] = s
+
+        waiting, issued = list(LOADS), []
+        before = None
+        for s, (run, engines, tasks, products) in enumerate(STEPS):
+            while waiting:
+                if buffered(waiting[0]):
+                    if len(issued) >= INPUT_BUFS and last_use[issued[-INPUT_BUFS]] >= s:
                         break
-                    issued.append(loads[0])
-                load(loads.pop(0))
-            cur = transposes(run) if run else None
-            while pend:
-                drain(*pend.pop(0))
-            if prev:
-                quantize(prev)
-            prev = (empty(cur[0], engs), len(cur[0]), cur[1], cur[2]) if cur else None
-            for m in ms:
-                mtask(m)
-            for v in vs:
-                vtask(v)
-        assert not prev and not pend and not loads
+                    issued.append(waiting[0])
+                load(waiting.pop(0))
+            banks = transpose_run(run) if run else None
+            while full:
+                empty(*full.pop(0))
+            if before:
+                quantize_run(*before)
+            before = (run, copy_run(banks, engines)) if run else None
+            for name in products:
+                product(name)
+            for name in tasks:
+                task(name)

from contextlib import ExitStack

import concourse.mybir as mybir
from concourse.masks import make_identity

F32 = mybir.dt.float32
BF16 = mybir.dt.bfloat16
U32 = mybir.dt.uint32
U8 = mybir.dt.uint8
E4M3 = mybir.dt.float8_e4m3fn_x4
E5M2 = mybir.dt.float8_e5m2_x4
MULT = mybir.AluOpType.mult
ADD = mybir.AluOpType.add
SUB = mybir.AluOpType.subtract

TOKENS, DIM, RANK, HEADS, HEAD = 512, 2048, 512, 16, 192
NOPE, ROPE = 2048, 1024
FEATURES = 4096
WIDTH = ROPE + RANK
FLOPS = 2 * (TOKENS * FEATURES * RANK + 2 * TOKENS * WIDTH * DIM)
BYTES = (
    2 * (TOKENS * DIM + DIM * WIDTH + RANK * FEATURES + TOKENS * (FEATURES + ROPE) + 256 * 64 + RANK)
    + 4 * (TOKENS * RANK + 2 * TOKENS)
    + 4 * (TOKENS * DIM + DIM * WIDTH)
)

INPUT_BUFS = 10
OUT_BUFS = 6
SPLIT_BUFS = 3
DZ2_BUFS = 3
TURNED_BUFS = 3
TURN_BANKS = 4
PRODUCT_BANKS = 3

LOADS = [
    "t", "g 0", "w 4", "g 2", "w 5", "w 6", "w 7", "g 1", "w 0", "k 5", "s", "x 0", "g 3", "w 1",
    "w 2", "w 3", "a 0", "x 1", "k 12", "a 2", "k 2", "c", "a 1", "x 3", "a 3", "k 1", "x 2", "k 0",
    "k 3", "k 7", "k 10", "k 6", "k 4", "k 15", "k 13", "k 14", "k 11", "k 8", "k 9",
]

STEPS = [
    ("W 4", "SS", ["tables", "turn 0", "sum 0", "turn 2", "sum 2"], []),
    ("W 5", "SS", ["turn 1"], []),
    ("Z 2 0", "SS", [], []),
    ("W 6", "SS", [], ["gain S"]),
    ("W 7", "SS", ["sum 1", "xlay 0 S"], []),
    ("Z 0 0", "VS", ["turn 3"], []),
    ("F 0", "SS", ["xquant 0"], []),
    ("W 0", "SS", [], []),
    ("W 1", "SS", ["sum 3"], []),
    ("W 2", "SS", [], []),
    ("Z 0 1", "SS", [], []),
    ("W 3", "SS", ["xlay 1 V"], []),
    ("Z 2 1", "SS", ["xhat 0", "split 5 V"], []),
    ("Z 1 0", "SS", ["zlay 1 S", "xquant 1", "xhat 2", "norm1 0"], ["dh 0"]),
    ("Z 1 1", "SV", ["split 12 V", "zquant 1", "zlay 0 S"], []),
    ("Z 3 0", "SS", ["zquant 0", "norm1 2", "norm2 0", "norm2 2", "norm3 0", "xlay 2 S", "norm3 2"], ["dh 2"]),
    ("", "", ["xquant 2", "xlay 3 V"], []),
    ("K 0 0", "SS", [], ["A 4 S S", "dh 1"]),
    ("Z 3 1", "SS", ["xquant 3", "xhat 1", "norm1 1", "norm4 0"], ["A 5 S S"]),
    ("K 0 1", "SS", [], []),
    ("K 0 2", "SS", ["norm2 1"], ["A 8 S S"]),
    ("", "", ["norm1 3"], ["dh 3", "A 0 S S"]),
    ("K 1 0", "SS", ["xhat 3", "norm4 2", "norm2 3"], ["A 6 S V", "A 12 V S"]),
    ("K 1 1", "VS", ["norm3 1"], ["A 7 V S", "A 13 S S"]),
    ("K 2 0", "VS", ["norm3 3"], ["A 1 V S", "A 9 S S"]),
    ("F 1", "SS", ["norm4 1"], ["A 2 V V", "A 10 S V"]),
    ("K 3 0", "SS", ["norm4 3"], []),
    ("K 2 1", "VS", ["zlay 2 V"], ["A 3 S S", "A 11 S S"]),
    ("D", "VS", ["zquant 2"], ["A 14 S V", "A 15 V S"]),
    ("K 2 2", "SS", [], []),
    ("K 1 2", "SV", [], ["l 0 S", "l 1 S", "l 2 V"]),
    ("K 3 1", "SV", [], ["l 3 S", "l 4 S", "l 5 V"]),
    ("K 3 2", "SS", [], ["l 6 S", "l 7 V"]),
    ("", "", [], ["o 0 3 S", "o 1 3 S", "l 8 V", "l 9 V", "o 1 1 S", "l 10 V", "o 0 1 S", "l 11 V", "o 2 3 S", "l 12 V", "l 13 S", "o 3 3 V", "o 0 2 V", "o 1 2 S", "o 2 1 V", "l 14 V", "l 15 S", "o 1 0 V", "o 0 0 S", "o 2 0 V", "o 3 0 S", "o 3 1 S", "o 3 2 S", "o 2 2 S"]),
    ("", "", [], []),
]


def tile_mla_pa_v_kernel(
    tc, x, wkv_a_w, wkv_a_b, kvn_g, kvn_b, wk_w, wk_b, wv_w, wv_b, cos, sin, c_lat, mu, rstd, grad_0, grad_1, out_0, out_1
):
    nc = tc.nc
    x_rows = x.flatten_outer_dims().rearrange("(p j) w -> p j w", j=4)
    grad_0_rows = grad_0.rearrange("b s h d -> (b s) (h d)").rearrange("(p j) w -> p j w", j=4)
    grad_1_rows = grad_1.rearrange("b s h d -> (b s) (h d)").rearrange("(p j) w -> p j w", j=4)
    c_lat_rows = c_lat.flatten_outer_dims().rearrange("(p j) w -> p j w", j=4)
    mu_rows = mu.flatten_outer_dims().rearrange("(p j) o -> p (j o)", j=4)
    rstd_rows = rstd.flatten_outer_dims().rearrange("(p j) o -> p (j o)", j=4)
    out_0_rows = out_0.flatten_outer_dims().rearrange("(p j) w -> p j w", j=4)
    out_1_rows = out_1.rearrange("(m p) w -> p m w", p=128)
    cos_rows = cos.rearrange("(q j) w -> q j w", j=4)
    sin_rows = sin.rearrange("(q j) w -> q j w", j=4)

    with ExitStack() as ctx:
        keep = ctx.enter_context(tc.tile_pool(name="keep", bufs=1))
        inputs = ctx.enter_context(tc.tile_pool(name="inputs", bufs=INPUT_BUFS))
        outputs = ctx.enter_context(tc.tile_pool(name="outputs", bufs=OUT_BUFS))
        turned = ctx.enter_context(tc.tile_pool(name="turned", bufs=TURNED_BUFS))
        work = ctx.enter_context(tc.tile_pool(name="work", bufs=2))
        psum = ctx.enter_context(tc.psum_pool(name="psum", bufs=1))

        def kept(name, shape, dtype):
            return keep.tile(shape, dtype, name=name, align_bytes=64)

        identity = kept("identity", [128, 128], F32)
        make_identity(nc, identity[:])
        ones = kept("ones", [128, 128], BF16)
        nc.gpsimd.memset(ones[:], 1.0)
        gain_row = kept("gain_row", [128, RANK], BF16)
        nc.gpsimd.memset(gain_row[:], 0.0)
        cos_in = kept("cos_in", [128, 4, 32], BF16)
        sin_in = kept("sin_in", [128, 4, 32], BF16)
        mu_col = kept("mu_col", [128, 4], F32)
        rstd_col = kept("rstd_col", [128, 4], F32)
        rstd_mean_col = kept("rstd_mean_col", [128, 4], F32)
        w2_codes = kept("w2_codes", [128, 8, RANK], U32)
        w2_scales = kept("w2_scales", [128, 8, RANK], U8)
        x_codes = kept("x_codes", [128, DIM], U32)
        x_scales = kept("x_scales", [128, DIM], U8)
        wkv_codes = kept("wkv_codes", [128, 3, DIM], U32)
        wkv_scales = kept("wkv_scales", [128, 3, DIM], U8)
        dz1_token_codes = kept("dz1_token_codes", [128, WIDTH], U32)
        dz1_token_scales = kept("dz1_token_scales", [128, WIDTH], U8)
        rope_codes = kept("rope_codes", [128, 4, 2, 128], U32)
        rope_scales = kept("rope_scales", [128, 4, 2, 128], U8)
        latent_codes = kept("latent_codes", [128, 4, 128], U32)
        latent_scales = kept("latent_scales", [128, 4, 128], U8)
        g0 = kept("g0", [128, 4, HEADS * HEAD], BF16)
        xhat = kept("xhat", [128, 4, RANK], F32)
        dc = kept("dc", [128, 4, RANK], BF16)
        gain = kept("gain", [128, RANK], F32)
        cos_pairs = kept("cos_pairs", [128, 4, 32, 2], BF16)
        sin_pairs = kept("sin_pairs", [128, 4, 32, 2], BF16)
        means = kept("means", [128, 4, 2], F32)

        def copy(engine, out, in_):
            if engine == "V":
                nc.vector.tensor_copy(out=out, in_=in_)
            else:
                nc.scalar.copy(out=out, in_=in_)

        loaded = {}

        def load(name):
            k, *rest = name.split()
            i = int(rest[0]) if rest else 0
            if k == "x":
                t = outputs.tile([128, 4, 512], BF16, name="out", align_bytes=64)
                loaded[name] = t
                nc.sync.dma_start(out=t[:], in_=x_rows[:, :, 512 * i : 512 * i + 512])
            elif k in "wak":
                t = inputs.tile([128, 2048], BF16, name="input", align_bytes=64)
                loaded[name] = t
                if k == "k":
                    nc.sync.dma_start(out=t[:, 0:WIDTH], in_=wkv_a_w[128 * i : 128 * i + 128, :])
                elif k == "a":
                    nc.sync.dma_start(out=t[:], in_=grad_1_rows[:, i, :])
                else:
                    w = wk_w if i < 4 else wv_w
                    nc.sync.dma_start(out=t[:], in_=w[128 * (i % 4) : 128 * (i % 4) + 128, :])
            elif k == "g":
                nc.sync.dma_start(out=g0[:, i, :], in_=grad_0_rows[:, i, :])
            elif k == "c":
                nc.sync.dma_start(out=xhat[:], in_=c_lat_rows)
            elif k == "t":
                for half in (slice(0, 64), slice(64, 128)):
                    nc.sync.dma_start(out=cos_in[half], in_=cos_rows)
                    nc.sync.dma_start(out=sin_in[half], in_=sin_rows)
            elif k == "s":
                nc.sync.dma_start(out=mu_col[:], in_=mu_rows)
                nc.sync.dma_start(out=rstd_col[:], in_=rstd_rows)
                nc.sync.dma_start(out=gain_row[0:1, :], in_=kvn_g.rearrange("(o w) -> o w", o=1))

        def buffered(name):
            return name[0] in "wak"

        dz2, split = {}, {}

        def run_inputs(run):
            k, *a = run.split()
            if k == "W":
                first = 4 * (int(a[0]) // 4)
                return ["w %d" % (first + i) for i in range(4)]
            if k == "K":
                return ["k %d" % (4 * int(a[0]) + i) for i in range(4)]
            return ["a " + a[0]] if k == "Z" and a[1] == "1" else []

        def words(rows, g):
            return rows.bitcast(F32)[:, 256 * g : 256 * g + 256].rearrange("p (w u) -> p u w", u=2)

        def run_blocks(run):
            k, *a = run.split()
            a = [int(z) for z in a]
            if k == "W":
                return [words(loaded[name][:], a[0] % 4) for name in run_inputs(run)]
            if k == "K":
                return [split[name][:, a[1], :, :] if name in split else words(loaded[name][:], a[1]) for name in run_inputs(run)]
            if k == "Z":
                rows = loaded["a %d" % a[0]][:] if a[1] else g0[:, a[0], 0:NOPE]
                return [words(rows, g) for g in range(4)]
            if k == "F":
                return [words(g0[:, 2 * a[0] + i, NOPE : NOPE + ROPE], g) for i in range(2) for g in range(2)]
            return [words(dc[:, j, :], 0) for j in range(4)]

        def run_operand(run):
            k, *a = run.split()
            a = [int(z) for z in a]
            if k == "W":
                return w2_codes[:, a[0], :], w2_scales[:, a[0], :], E4M3
            if k == "K":
                cols = slice(512 * a[0], 512 * a[0] + 512)
                return wkv_codes[:, a[1], cols], wkv_scales[:, a[1], cols], E4M3
            if k == "Z":
                j, h = a
                if j not in dz2:
                    codes = work.tile([128, 8, 128], U32, name="dz2_codes", bufs=DZ2_BUFS, align_bytes=64)
                    scales = work.tile([128, 8, 128], U8, name="dz2_scales", bufs=DZ2_BUFS, align_bytes=64)
                    dz2[j] = (codes, scales)
                codes, scales = [t[:, 4 * h : 4 * h + 4, :].rearrange("p g n -> p (g n)") for t in dz2[j]]
                return codes, scales, E5M2
            if k == "F":
                tiles = slice(2 * a[0], 2 * a[0] + 2)
                codes, scales = [t[:, tiles, :, :].rearrange("p j g n -> p (j g n)") for t in (rope_codes, rope_scales)]
                return codes, scales, E5M2
            codes, scales = [t[:].rearrange("p j n -> p (j n)") for t in (latent_codes, latent_scales)]
            return codes, scales, E5M2

        def transpose_run(run):
            blocks = run_blocks(run)
            banks = []
            for b in range(2):
                bank = psum.tile([128, 2, 2, 128], F32, name="turn", bufs=TURN_BANKS)
                banks.append(bank)
                for a in range(2):
                    for u in range(2):
                        nc.tensor.transpose(bank[:, a, u, :], blocks[2 * b + a][:, u, :], identity[:])
            return banks

        def copy_run(banks, engines):
            rows = turned.tile([128, 4, 128, 4], BF16, name="rows", align_bytes=64)
            for b in range(2):
                copy(engines[b], rows[:, 2 * b : 2 * b + 2, :, :].bitcast(F32), banks[b][:].rearrange("p a u n -> p a n u"))
            return rows

        def quantize_run(run, rows):
            codes, scales, fmt = run_operand(run)
            nc.vector.quantize_mx(out=codes.bitcast(fmt), scales=scales, in_=rows[:].rearrange("p a n t -> p (a n t)"))

        dh, beside, halves, norm = {}, {}, {}, {}

        def task(name):
            k, *a = name.split()
            i = int(a[0]) if a else 0
            if k == "tables":
                for e in range(2):
                    nc.vector.tensor_copy(out=cos_pairs[:, :, :, e], in_=cos_in[:])
                nc.vector.tensor_scalar(out=sin_pairs[:, :, :, 0], in0=sin_in[:], scalar1=-1.0, scalar2=None, op0=MULT)
                nc.vector.tensor_copy(out=sin_pairs[:, :, :, 1], in_=sin_in[:])
            elif k == "turn":
                pairs = g0[:, i, :].rearrange("p (h w) -> p h w", w=HEAD)[:, :, 128:HEAD]
                halves[i] = []
                for table in (cos_pairs, sin_pairs):
                    half = work.tile([128, HEADS, 64], F32, name="half", tag="f32", bufs=3)
                    halves[i].append(half)
                    row = table[:, i, :, :].rearrange("p w e -> p (w e)")
                    nc.vector.tensor_tensor(out=half[:], in0=pairs, in1=row.unsqueeze(1).to_broadcast([128, HEADS, 64]), op=MULT)
            elif k == "sum":
                by_cos, by_sin = [half[:].rearrange("p h (w e) -> p h w e", e=2) for half in halves[i]]
                pairs = g0[:, i, :].rearrange("p (h w) -> p h w", w=HEAD)[:, :, 128:HEAD]
                nc.vector.tensor_tensor(out=pairs.rearrange("p h (w e) -> p h w e", e=2), in0=by_cos, in1=by_sin[:, :, :, ::-1], op=ADD)
            elif k in ("xlay", "zlay"):
                if k == "xlay":
                    cols = loaded["x %d" % i][:]
                else:
                    cols = g0[:, :, NOPE + 512 * i : NOPE + 512 * i + 512] if i < 2 else dc[:]
                tokens = work.tile([128, 512, 4], BF16, name="tokens", align_bytes=64)
                beside[(k[0], i)] = tokens
                copy(a[1], tokens[:].rearrange("p (c i) j -> p c j i", i=4), cols.rearrange("p j (c i) -> p c j i", i=4))
            elif k in ("xquant", "zquant"):
                codes, scales, fmt = (x_codes, x_scales, E4M3) if k == "xquant" else (dz1_token_codes, dz1_token_scales, E5M2)
                cols = slice(512 * i, 512 * i + 512)
                nc.vector.quantize_mx(out=codes[:, cols].bitcast(fmt), scales=scales[:, cols], in_=beside[(k[0], i)][:].rearrange("p c j -> p (c j)"))
            elif k == "split":
                t = inputs.tile([128, 3, 2, 128], F32, name="split", bufs=SPLIT_BUFS, align_bytes=64)
                split["k %d" % i] = t
                copy(a[1], t[:], loaded["k %d" % i][:].bitcast(F32)[:, 0 : WIDTH // 2].rearrange("p (g w u) -> p g u w", g=3, u=2))
            elif k == "xhat":
                if i == 0:
                    nc.vector.tensor_scalar(out=rstd_mean_col[:], in0=rstd_col[:], scalar1=1.0 / RANK, scalar2=None, op0=MULT)
                nc.vector.tensor_scalar(out=xhat[:, i, :], in0=xhat[:, i, :], scalar1=mu_col[:, i : i + 1], scalar2=rstd_col[:, i : i + 1], op0=SUB, op1=MULT)
            elif k == "norm1":
                t = work.tile([128, 2, RANK], F32, name="norm", tag="f32", bufs=3)
                norm[i] = (t[:, 0, :], t[:, 1, :])
                nc.vector.scalar_tensor_tensor(out=norm[i][0], in0=dh[i][:], scalar=rstd_mean_col[:, i : i + 1], in1=gain[:], op0=MULT, op1=MULT, accum_out=means[:, i, 0:1])
                if len(norm) == 4:
                    dh_done.append(True)
            elif k == "norm2":
                nc.vector.scalar_tensor_tensor(out=norm[i][1], in0=norm[i][0], scalar=1.0, in1=xhat[:, i, :], op0=MULT, op1=MULT, accum_out=means[:, i, 1:2])
            elif k == "norm3":
                nc.vector.tensor_scalar(out=norm[i][1], in0=xhat[:, i, :], scalar1=means[:, i, 1:2], scalar2=means[:, i, 0:1], op0=MULT, op1=ADD)
            elif k == "norm4":
                nc.vector.scalar_tensor_tensor(out=dc[:, i, :], in0=norm[i][0], scalar=float(RANK), in1=norm[i][1], op0=MULT, op1=SUB)

        full, dh_done, staged = [], [], {}
        late_banks = [0]

        def matmul_mx(out, left, right, start, stop):
            (l, l_scales, l_fmt), (r, r_scales, r_fmt) = left, right
            nc.tensor.matmul_mx(out=out, lhsT=l.bitcast(l_fmt), lhsT_scale=l_scales, rhs=r.bitcast(r_fmt), rhs_scale=r_scales, start=start, stop=stop)

        def product_bank():
            if len(full) == PRODUCT_BANKS + len(dh_done):
                empty(*full.pop(0))
            if dh_done:
                late_banks[0] += 1
            if late_banks[0] % (PRODUCT_BANKS + 1) == PRODUCT_BANKS:
                bank = psum.tile([128, 512], F32, name="dh")
            else:
                bank = psum.tile([128, 512], F32, name="product", bufs=PRODUCT_BANKS)
            return bank

        def product(name):
            k, *a = name.split()
            engines = [z for z in a if z in "VS"]
            a = [int(z) for z in a if z not in "VS"]
            if k == "gain":
                bank = product_bank()
                nc.tensor.matmul(bank[:], ones[:], gain_row[:], start=True, stop=True)
                full.append((bank, None, engines[0]))
            elif k == "dh":
                bank = psum.tile([128, 512], F32, name="dh")
                dh[a[0]] = bank
                codes, scales = dz2[a[0]]
                for g in range(8):
                    matmul_mx(bank[:], (codes[:, g, :], scales[:, g, :], E5M2), (w2_codes[:, g, :], w2_scales[:, g, :], E4M3), g == 0, g == 7)
            elif k in "Al":
                rows = slice(128 * a[0], 128 * a[0] + 128)
                for n in (0, 1) if k == "A" else (2,):
                    bank = product_bank()
                    cols = slice(512 * n, 512 * n + 512)
                    matmul_mx(bank[:], (x_codes[:, rows], x_scales[:, rows], E4M3), (dz1_token_codes[:, cols], dz1_token_scales[:, cols], E5M2), True, True)
                    full.append((bank, (k, a[0], n), engines[n % 2]))
            elif k == "o":
                n, j = a
                bank = product_bank()
                cols = slice(512 * n, 512 * n + 512)
                for g in range(3):
                    left = (rope_codes[:, j, g, :], rope_scales[:, j, g, :], E5M2) if g < 2 else (latent_codes[:, j, :], latent_scales[:, j, :], E5M2)
                    matmul_mx(bank[:], left, (wkv_codes[:, g, cols], wkv_scales[:, g, cols], E4M3), g == 0, g == 2)
                full.append((bank, (k, j, n), engines[0]))

        def empty(bank, place, engine):
            if place is None:
                copy(engine, gain[:], bank[:])
                return
            k, i, n = place
            pair, side = {"A": ((k, i), n), "l": ((k, i // 2), i % 2), "o": ((k, i, n // 2), n % 2)}[k]
            if pair not in staged:
                t = outputs.tile([128, 2, 512], F32, name="out", align_bytes=64)
                staged[pair] = [t]
            t = staged[pair][0]
            copy(engine, t[:, side, :], bank[:])
            staged[pair].append(side)
            if len(staged[pair]) == 3:
                if k == "A":
                    nc.sync.dma_start(out=out_1_rows[:, i, 0:ROPE], in_=t[:].rearrange("p a w -> p (a w)"))
                elif k == "l":
                    nc.sync.dma_start(out=out_1_rows[:, i // 2 * 2 : i // 2 * 2 + 2, ROPE:WIDTH], in_=t[:])
                else:
                    nc.sync.dma_start(out=out_0_rows[:, i, 1024 * (n // 2) : 1024 * (n // 2) + 1024], in_=t[:].rearrange("p a w -> p (a w)"))

        ctx.enter_context(tc.manual_schedule())

        split_names = ["k " + name.split()[1] for step in STEPS for name in step[2] if name.startswith("split")]
        last_use = {}
        for s, (run, engines, tasks, products) in enumerate(STEPS):
            for name in run_inputs(run) if run else []:
                if name not in split_names:
                    last_use[name] = s
            for name in tasks:
                if name.startswith("split"):
                    last_use["k " + name.split()[1]] = s

        waiting, issued = list(LOADS), []
        before = None
        for s, (run, engines, tasks, products) in enumerate(STEPS):
            while waiting:
                if buffered(waiting[0]):
                    if len(issued) >= INPUT_BUFS and last_use[issued[-INPUT_BUFS]] >= s:
                        break
                    issued.append(waiting[0])
                load(waiting.pop(0))
            banks = transpose_run(run) if run else None
            while full:
                empty(*full.pop(0))
            if before:
                quantize_run(*before)
            before = (run, copy_run(banks, engines)) if run else None
            for name in products:
                product(name)
            for name in tasks:
                task(name)
